import numpy as np
import ml_dtypes


def mxq(x, axis, fmt="e4m3"):
    dtype, down = {"e4m3": (ml_dtypes.float8_e4m3fn, 7), "e5m2": (ml_dtypes.float8_e5m2, 14)}[fmt]
    v = np.moveaxis(np.asarray(x, np.float32).astype(ml_dtypes.bfloat16).astype(np.float64), axis, -1)
    blocks = v.reshape(v.shape[:-1] + (-1, 32))
    amax = np.abs(blocks).max(-1, keepdims=True)
    byte = np.maximum(np.where(amax > 0, np.frexp(amax)[1] - 1 + 127, 0) - down, 1)
    scale = np.exp2(byte - 127.0)
    codes = (blocks / scale).astype(np.float32).astype(dtype).astype(np.float64)
    return np.moveaxis((codes * scale).reshape(v.shape), -1, axis)


WIDE = False


def mx_kscale(k):
    if not WIDE:
        return np.ones(k)
    levels = np.array([10, -10, 5, -5, 0])
    a = np.random.permutation(np.resize(levels, k // 512 * 4)).reshape(k // 512, 4)
    idx = np.arange(k)
    return np.exp2(a[idx // 512, idx % 128 // 32])


BF16 = ml_dtypes.bfloat16


def bf(x):
    return np.asarray(x, np.float32).astype(BF16)


def f64(x):
    return np.asarray(x).astype(np.float64)


N, D, H = 1024, 2048, 1024
H2 = H + H
LN_EPS = 1e-5
ERF_TERMS = 120


def erf(x):
    a = np.clip(x, -6.0, 6.0)
    term = a
    total = a
    for n in range(1, ERF_TERMS):
        term = term * (2.0 * a * a / (2.0 * n + 1.0))
        total = total + term
    return 2.0 / np.sqrt(np.pi) * np.exp(-a * a) * total


def gelu(v):
    return 0.5 * v * (1.0 + erf(v / np.sqrt(2.0)))


def layernorm(x, g, b):
    m = x.mean(-1, keepdims=True)
    v = np.square(x - m).mean(-1, keepdims=True)
    return (x - m) / np.sqrt(v + LN_EPS) * g + b


def setup_inputs():
    s, t = mx_kscale(D), mx_kscale(H2)
    return {
        "z": bf(np.random.standard_normal((N, D)) * s),
        "attention_out": bf(np.random.standard_normal((N, H)) * t[H:]),
        "Wz": bf(np.random.standard_normal((H, D)) / np.sqrt(D) / s),
        "bz": bf(0.1 * np.random.standard_normal(H)),
        "gz": bf((1.0 + 0.1 * np.random.standard_normal(H)) * t[:H]),
        "bz_ln": bf(0.1 * np.random.standard_normal(H) * t[:H]),
        "w1_deq": bf(np.random.standard_normal((H, H2)) / np.sqrt(H2) / t),
        "b1": bf(0.1 * np.random.standard_normal(H)),
        "g1": bf(1.0 + 0.1 * np.random.standard_normal(H)),
        "b1_ln": bf(0.1 * np.random.standard_normal(H)),
    }


def reference(z, attention_out, Wz, bz, gz, bz_ln, w1_deq, b1, g1, b1_ln):
    z_proj = layernorm((mxq(f64(z), 1, "e4m3") @ mxq(f64(Wz), 1, "e4m3").T) + f64(bz), f64(gz), f64(bz_ln))
    combined = np.concatenate([z_proj, f64(attention_out)], axis=-1)
    y = (mxq(combined, 1, "e4m3") @ mxq(f64(w1_deq), 1, "e4m3").T) + f64(b1)
    return gelu(layernorm(y, f64(g1), f64(b1_ln)))

@@ -1,0 +1,312 @@
+from contextlib import ExitStack
+
+import concourse.mybir as mybir
+from concourse.masks import make_identity
+
+F32 = mybir.dt.float32
+BF16 = mybir.dt.bfloat16
+U32 = mybir.dt.uint32
+U8 = mybir.dt.uint8
+I32 = mybir.dt.int32
+FP8X4 = mybir.dt.float8_e4m3fn_x4
+ALU = mybir.AluOpType
+ACT = mybir.ActivationFunctionType
+
+P = 128
+N_TOK = 1024
+D_IN = 2048
+H = 1024
+LN_EPS = 1e-5
+FLOPS = 2 * N_TOK * D_IN * H + 2 * N_TOK * (2 * H) * H
+
+VEC_EXIT_EVERY = 0
+
+
+def tile_synapsemodel_pa_kernel(tc, z, attention_out, Wz, bz, gz, bz_ln, w1_deq, b1, g1, b1_ln, out):
+    nc = tc.nc
+    with ExitStack() as ctx:
+        const = ctx.enter_context(tc.tile_pool(name="const", bufs=1))
+        keep = ctx.enter_context(tc.tile_pool(name="keep", bufs=1))
+        raw = ctx.enter_context(tc.tile_pool(name="raw", bufs=10))
+        rawa = ctx.enter_context(tc.tile_pool(name="rawa", bufs=4))
+        stage = ctx.enter_context(tc.tile_pool(name="stage", bufs=4))
+        stagea = ctx.enter_context(tc.tile_pool(name="stagea", bufs=3))
+        rows1 = ctx.enter_context(tc.tile_pool(name="rows1", bufs=6))
+        rows2 = ctx.enter_context(tc.tile_pool(name="rows2", bufs=2))
+        rows3 = ctx.enter_context(tc.tile_pool(name="rows3", bufs=3))
+        junkp = ctx.enter_context(tc.tile_pool(name="junkp", bufs=2))
+        plan = ctx.enter_context(tc.tile_pool(name="plan", bufs=2))
+        small = ctx.enter_context(tc.tile_pool(name="small", bufs=4))
+        ps_t = ctx.enter_context(tc.psum_pool(name="ps_t", bufs=4))
+        ps_a = ctx.enter_context(tc.psum_pool(name="ps_a", bufs=4))
+
+        ident = const.tile([P, P], F32, name="ident")
+        make_identity(nc, ident[:])
+        identb = const.tile([P, P], BF16, name="identb")
+        nc.vector.tensor_copy(out=identb[:], in_=ident[:])
+        mhalf = const.tile([P, 1], F32, name="mhalf")
+        nc.vector.memset(mhalf[:], -0.5)
+
+        vrows1 = const.tile([P, 512], BF16, name="vrows1")
+        nc.vector.memset(vrows1[:].bitcast(I32), 0)
+        grows = const.tile([P, 256], BF16, name="grows")
+        nc.vector.memset(grows[:].bitcast(I32), 0)
+        vrows2 = const.tile([P, 512], BF16, name="vrows2")
+        nc.vector.memset(vrows2[:].bitcast(I32), 0)
+        nc.scalar.dma_start(out=vrows1[0:2, :], in_=bz.rearrange("(a c) -> a c", a=2))
+        nc.scalar.dma_start(out=grows[0:4, :], in_=gz.rearrange("(a c) -> a c", a=4))
+        nc.scalar.dma_start(out=grows[4:8, :], in_=bz_ln.rearrange("(a c) -> a c", a=4))
+        nc.gpsimd.dma_start(out=vrows2[2:4, :], in_=b1.rearrange("(a c) -> a c", a=2))
+        nc.gpsimd.dma_start(out=vrows2[4:6, :], in_=g1.rearrange("(a c) -> a c", a=2))
+        nc.gpsimd.dma_start(out=vrows2[6:8, :], in_=b1_ln.rearrange("(a c) -> a c", a=2))
+
+        wz_v = Wz.rearrange("(a q e) k -> a e q k", q=P, e=2)
+        order = (
+            [("W", j) for j in range(4)] + [("z", 0), ("z", 1)] + [("W", j) for j in range(4, 8)]
+            + [("z", 2), ("z", 3)] + [("w", j) for j in range(8)] + [("a", i) for i in range(4)]
+            + [("z", i) for i in range(4, 8)] + [("a", i) for i in range(4, 8)]
+        )
+        loaded = {}
+        for kind, idx in order:
+            if kind == "a":
+                t = rawa.tile([P, H], BF16, tag="rawa")
+                src = attention_out[idx * P:(idx + 1) * P, :]
+            else:
+                t = raw.tile([P, D_IN], BF16, tag="raw")
+                if kind == "W":
+                    src = wz_v[idx // 2, idx % 2]
+                elif kind == "z":
+                    src = z[idx * P:(idx + 1) * P, :]
+                else:
+                    src = w1_deq[idx * P:(idx + 1) * P, :]
+            nc.sync.dma_start(out=t[:], in_=src)
+            loaded[(kind, idx)] = t
+
+        zq = keep.tile([P, 8 * 512], U32, name="zq", align_bytes=64)
+        zs = keep.tile([P, 8 * 512], U8, name="zs", align_bytes=64)
+        wq = keep.tile([P, 4 * 1024], U32, name="wq", align_bytes=64)
+        ws = keep.tile([P, 4 * 1024], U8, name="ws", align_bytes=64)
+        vq = keep.tile([P, 4 * 1024], U32, name="vq", align_bytes=64)
+        vs = keep.tile([P, 4 * 1024], U8, name="vs", align_bytes=64)
+        pq = keep.tile([P, 4 * 512], U32, name="pq", align_bytes=64)
+        pscl = keep.tile([P, 4 * 512], U8, name="pscl", align_bytes=64)
+        aq = keep.tile([P, 8 * 256], U32, name="aq", align_bytes=64)
+        ascl = keep.tile([P, 8 * 256], U8, name="ascl", align_bytes=64)
+
+        bc = const.tile([P, 4 * 1024], BF16, name="bc")
+        gb = const.tile([P, 16], F32, name="gb")
+        counter = [0]
+
+        def exit_copy(dst, src):
+            counter[0] += 1
+            if VEC_EXIT_EVERY and counter[0] % VEC_EXIT_EVERY == 0:
+                nc.vector.tensor_copy(out=dst, in_=src)
+            else:
+                nc.scalar.copy(out=dst, in_=src)
+
+        def bcast(r):
+            pb = ps_t.tile([P, 512], F32, tag="tp")
+            nc.tensor.matmul(pb[:], lhsT=identb[:, r:r + 1].to_broadcast([P, P]), rhs=(vrows1 if r < 2 else vrows2)[:], start=True, stop=True)
+            dst = bc[:, r * 512:(r + 1) * 512]
+            if r < 2:
+                nc.vector.tensor_copy(
+                    out=dst.rearrange("p (u e q) -> p u e q", u=2, e=2),
+                    in_=pb[:].rearrange("p (u q e) -> p u e q", u=2, e=2),
+                )
+            else:
+                nc.vector.tensor_copy(out=dst, in_=pb[:])
+
+        def consts_a():
+            bcast(0)
+            bcast(1)
+            g32 = const.tile([P, 256], F32, name="g32")
+            nc.vector.tensor_copy(
+                out=g32[:].rearrange("p (e q) -> p e q", e=2), in_=grows[:].rearrange("p (q e) -> p e q", e=2)
+            )
+            pg = ps_t.tile([P, 512], F32, tag="tp")
+            for e in range(2):
+                nc.tensor.transpose(pg[:, e * P:(e + 1) * P], g32[:, e * P:(e + 1) * P], ident[:])
+            nc.vector.tensor_copy(
+                out=gb[:].rearrange("p (w a e) -> p w a e", w=2, e=2),
+                in_=pg[:, 0:256].rearrange("p (e r) -> p e r", e=2)[:, :, 0:8].rearrange("p e (w a) -> p w a e", w=2),
+            )
+
+        def consts_b():
+            for r in range(2, 8):
+                bcast(r)
+
+        def do_input(kind, idx):
+            t = loaded[(kind, idx)]
+            width = H if kind == "a" else D_IN
+            words = t[:].bitcast(F32)
+            if kind == "a":
+                grouped = stagea.tile([P, width], BF16, tag="grpa", align_bytes=64)
+            else:
+                grouped = stage.tile([P, width], BF16, tag="grp", align_bytes=64)
+            gw = grouped[:].bitcast(F32)
+            for b in range(width // 1024):
+                xt = ps_t.tile([P, 512], F32, tag="tp")
+                for s in range(4):
+                    c0 = (4 * b + s) * P
+                    nc.tensor.transpose(xt[:, s * P:(s + 1) * P], words[:, c0:c0 + P], ident[:])
+                exit_copy(
+                    gw[:, b * 512:(b + 1) * 512].rearrange("p (g r u) -> p g r u", g=2, u=2),
+                    xt[:].rearrange("p (g u r) -> p g r u", g=2, u=2),
+                )
+            if kind == "z":
+                sl = slice(idx * 512, (idx + 1) * 512)
+                nc.vector.quantize_mx(out=zq[:, sl].bitcast(FP8X4), scales=zs[:, sl], in_=grouped[:])
+            elif kind == "a":
+                sl = slice(idx * 256, (idx + 1) * 256)
+                nc.vector.quantize_mx(out=aq[:, sl].bitcast(FP8X4), scales=ascl[:, sl], in_=grouped[:])
+            else:
+                cq, cs = (wq, ws) if kind == "W" else (vq, vs)
+                for g in range(4):
+                    sl = slice(g * 1024 + idx * P, g * 1024 + (idx + 1) * P)
+                    nc.vector.quantize_mx(
+                        out=cq[:, sl].bitcast(FP8X4), scales=cs[:, sl], in_=grouped[:, g * 512:(g + 1) * 512]
+                    )
+
+        def stats_tail(y, s):
+            nm = small.tile([P, 1], F32, tag="nm")
+            nc.vector.tensor_scalar(
+                out=nm[:], in0=s[:, 0:1], scalar1=s[:, 1:2], scalar2=-1.0 / H, op0=ALU.add, op1=ALU.mult
+            )
+            junk = junkp.tile([P, H], BF16, tag="junk")
+            ssq = small.tile([P, 1], F32, tag="ssq")
+            nc.scalar.activation(out=junk[:], in_=y[:], func=ACT.Square, bias=nm[:], scale=1.0, accum_out=ssq[:])
+            ve = small.tile([P, 1], F32, tag="ve")
+            nc.gpsimd.tensor_scalar(out=ve[:], in0=ssq[:], scalar1=1.0 / H, scalar2=LN_EPS, op0=ALU.mult, op1=ALU.add)
+            rstd = small.tile([P, 1], F32, tag="rstd")
+            nc.gpsimd.tensor_tensor(out=rstd[:], in0=ve[:], in1=mhalf[:], op=ALU.pow)
+            return nm, rstd
+
+        ys = {}
+        sums = {}
+
+        def m1(i, n):
+            acc = ps_a.tile([P, 512], F32, tag="acc")
+            for g in range(4):
+                sl = slice(i * 512 + g * P, i * 512 + (g + 1) * P)
+                sr = slice(g * 1024 + n * 512, g * 1024 + (n + 1) * 512)
+                nc.tensor.matmul_mx(
+                    out=acc[:], lhsT=zq[:, sl].bitcast(FP8X4), lhsT_scale=zs[:, sl],
+                    rhs=wq[:, sr].bitcast(FP8X4), rhs_scale=ws[:, sr], start=(g == 0), stop=(g == 3),
+                )
+            if n == 0:
+                y = rows1.tile([P, H], F32, tag="y1")
+                s = small.tile([P, 2], F32, tag="s")
+                ys[i] = y
+                sums[i] = s
+            nc.vector.scalar_tensor_tensor(
+                out=ys[i][:, n * 512:(n + 1) * 512], in0=acc[:], scalar=1.0, in1=bc[:, n * 512:(n + 1) * 512],
+                op0=ALU.mult, op1=ALU.add, accum_out=sums[i][:, n:n + 1],
+            )
+
+        def ep1(i):
+            y = ys[i]
+            nm, rstd = stats_tail(y, sums[i])
+            nc.gpsimd.tensor_scalar(out=y[:], in0=y[:], scalar1=nm[:], scalar2=rstd[:], op0=ALU.add, op1=ALU.mult)
+
+        def tproj(b):
+            for g in range(2):
+                planar = plan.tile([P, 4 * 512], BF16, tag="planar")
+                for t in range(4):
+                    j = 4 * g + t
+                    tp = ps_t.tile([P, 512], F32, tag="tp")
+                    for c in range(4):
+                        nc.tensor.transpose(tp[:, c * P:(c + 1) * P], ys[4 * b + c][:, j * P:(j + 1) * P], ident[:])
+                    nc.scalar.activation(
+                        out=planar[:, t * 512:(t + 1) * 512], in_=tp[:], func=ACT.Identity,
+                        scale=gb[:, j:j + 1], bias=gb[:, 8 + j:9 + j],
+                    )
+                gp = plan.tile([P, 4 * 512], BF16, tag="gp", align_bytes=64)
+                nc.vector.tensor_copy(
+                    out=gp[:].rearrange("p (c i t) -> p c t i", i=4, t=4),
+                    in_=planar[:].rearrange("p (t c i) -> p c t i", t=4, i=4),
+                )
+                sl = slice((2 * b + g) * 512, (2 * b + g + 1) * 512)
+                nc.vector.quantize_mx(out=pq[:, sl].bitcast(FP8X4), scales=pscl[:, sl], in_=gp[:])
+
+        def m2(i):
+            y = rows2.tile([P, H], F32, tag="y2")
+            s = small.tile([P, 2], F32, tag="s")
+            for n in range(2):
+                acc = ps_a.tile([P, 512], F32, tag="acc")
+                for g in range(4):
+                    if g < 2:
+                        c0 = (2 * (i // 4) + g) * 512 + (i % 4) * P
+                        lq, ls = pq, pscl
+                    else:
+                        c0 = i * 256 + (g - 2) * P
+                        lq, ls = aq, ascl
+                    sl = slice(c0, c0 + P)
+                    sr = slice(g * 1024 + n * 512, g * 1024 + (n + 1) * 512)
+                    nc.tensor.matmul_mx(
+                        out=acc[:], lhsT=lq[:, sl].bitcast(FP8X4), lhsT_scale=ls[:, sl],
+                        rhs=vq[:, sr].bitcast(FP8X4), rhs_scale=vs[:, sr], start=(g == 0), stop=(g == 3),
+                    )
+                nc.vector.scalar_tensor_tensor(
+                    out=y[:, n * 512:(n + 1) * 512], in0=acc[:], scalar=1.0,
+                    in1=bc[:, 1024 + n * 512:1024 + (n + 1) * 512],
+                    op0=ALU.mult, op1=ALU.add, accum_out=s[:, n:n + 1],
+                )
+            nm, rstd = stats_tail(y, s)
+            t2 = rows3.tile([P, H], F32, tag="t2")
+            nc.vector.scalar_tensor_tensor(
+                out=t2[:], in0=y[:], scalar=nm[:], in1=bc[:, 2048:3072], op0=ALU.add, op1=ALU.mult
+            )
+            nc.vector.scalar_tensor_tensor(
+                out=t2[:], in0=t2[:], scalar=rstd[:], in1=bc[:, 3072:4096], op0=ALU.mult, op1=ALU.add
+            )
+            nc.scalar.activation(out=t2[:], in_=t2[:], func=ACT.Gelu)
+            nc.sync.dma_start(out=out[i * P:(i + 1) * P, :], in_=t2[:])
+
+        for j in range(4):
+            do_input("W", j)
+        do_input("z", 0)
+        do_input("z", 1)
+        consts_a()
+        m1(0, 0)
+        m1(1, 0)
+        for j in range(4, 8):
+            do_input("W", j)
+        m1(0, 1)
+        ep1(0)
+        m1(1, 1)
+        ep1(1)
+        consts_b()
+        do_input("z", 2)
+        do_input("z", 3)
+        for i in (2, 3):
+            m1(i, 0)
+            m1(i, 1)
+            ep1(i)
+        for j in range(4):
+            do_input("w", j)
+        tproj(0)
+        for j in range(4, 8):
+            do_input("w", j)
+        for i in range(4):
+            do_input("a", i)
+        for i in (4, 5):
+            do_input("z", i)
+        for i in (4, 5):
+            m1(i, 0)
+            m1(i, 1)
+            ep1(i)
+        for i in (6, 7):
+            do_input("z", i)
+        for i in (6, 7):
+            m1(i, 0)
+            m1(i, 1)
+            ep1(i)
+        m2(0)
+        m2(1)
+        for i in range(4, 8):
+            do_input("a", i)
+        tproj(1)
+        m2(2)
+        m2(3)
+        for i in range(4, 8):
+            m2(i)

@@ -206,7 +206,7 @@ def tile_synapsemodel_pa_kernel(tc, z, attention_out, Wz, bz, gz, bz_ln, w1_deq,
         def ep1(i):
             y = ys[i]
             nm, rstd = stats_tail(y, sums[i])
-            nc.gpsimd.tensor_scalar(out=y[:], in0=y[:], scalar1=nm[:], scalar2=rstd[:], op0=ALU.add, op1=ALU.mult)
+            nc.vector.tensor_scalar(out=y[:], in0=y[:], scalar1=nm[:], scalar2=rstd[:], op0=ALU.add, op1=ALU.mult)
 
         def tproj(b):
             for g in range(2):

@@ -19,7 +19,72 @@ H = 1024
 LN_EPS = 1e-5
 FLOPS = 2 * N_TOK * D_IN * H + 2 * N_TOK * (2 * H) * H
 
-VEC_EXIT_EVERY = 0
+SCHEDULE = (
+    ("LD", "W", 0), ("LD", "W", 1), ("LD", "W", 2), ("LD", "W", 3), ("LD", "W", 4), ("LD", "W", 5),
+    ("LD", "W", 6), ("LD", "W", 7), ("LD", "z", 0), ("LD", "a", 0), ("LD", "z", 1), ("LD", "a", 1),
+    ("LD", "w", 0), ("LD", "w", 1), ("LD", "z", 2), ("LD", "a", 2), ("LD", "w", 2), ("LD", "w", 3),
+    ("LD", "z", 3), ("LD", "a", 3), ("LD", "w", 4), ("LD", "w", 5), ("LD", "w", 6), ("LD", "w", 7),
+    ("LD", "z", 4), ("LD", "a", 4), ("LD", "z", 5), ("LD", "a", 5), ("LD", "z", 6), ("LD", "a", 6),
+    ("LD", "z", 7), ("LD", "a", 7), ("CA",), ("T", "W", 0, 0), ("T", "W", 0, 1), ("EX", "W", 0, 0, "S"),
+    ("EX", "W", 0, 1, "V"), ("T", "W", 1, 0), ("Q", "W", 0), ("T", "W", 1, 1), ("CB", 2), ("EX", "W", 1, 0, "S"),
+    ("EX", "W", 1, 1, "V"), ("T", "W", 2, 0), ("Q", "W", 1), ("T", "W", 2, 1), ("CB", 3), ("EX", "W", 2, 0, "S"),
+    ("EX", "W", 2, 1, "V"), ("T", "W", 3, 0), ("T", "W", 3, 1), ("CB", 4), ("Q", "W", 2), ("EX", "W", 3, 0, "S"),
+    ("EX", "W", 3, 1, "V"), ("T", "W", 4, 0), ("T", "W", 4, 1), ("CB", 5), ("EX", "W", 4, 0, "S"), ("Q", "W", 3),
+    ("T", "W", 5, 0), ("EX", "W", 4, 1, "V"), ("T", "W", 5, 1), ("CB", 6), ("EX", "W", 5, 0, "S"), ("Q", "W", 4),
+    ("T", "W", 6, 0), ("EX", "W", 5, 1, "V"), ("T", "W", 6, 1), ("CB", 7), ("EX", "W", 6, 0, "S"), ("Q", "W", 5),
+    ("T", "W", 7, 0), ("EX", "W", 6, 1, "V"), ("T", "W", 7, 1), ("EX", "W", 7, 0, "S"), ("Q", "W", 6), ("T", "z", 0, 0),
+    ("EX", "W", 7, 1, "V"), ("T", "z", 0, 1), ("EX", "z", 0, 0, "S"), ("T", "a", 0, 0), ("Q", "W", 7), ("EX", "z", 0, 1, "S"),
+    ("EX", "a", 0, 0, "S"), ("Q", "z", 0), ("T", "z", 1, 0), ("T", "z", 1, 1), ("EX", "z", 1, 0, "S"), ("Q", "a", 0),
+    ("T", "a", 1, 0), ("M1", 0, 0), ("EX", "z", 1, 1, "S"), ("EX", "a", 1, 0, "S"), ("Q", "z", 1), ("M1", 0, 1),
+    ("Q", "a", 1), ("A1", 0, 0), ("T", "w", 0, 0), ("A1", 0, 1), ("T", "w", 0, 1), ("EX", "w", 0, 0, "S"),
+    ("NM1", 0), ("T", "w", 1, 0), ("EX", "w", 0, 1, "V"), ("T", "w", 1, 1), ("B1", 0), ("T", "z", 2, 0),
+    ("Q", "w", 0), ("T", "z", 2, 1), ("EX", "w", 1, 1, "V"), ("T", "a", 2, 0), ("EX", "w", 1, 0, "S"), ("R1", 0),
+    ("M1", 1, 0), ("EX", "z", 2, 0, "S"), ("Q", "w", 1), ("EX", "z", 2, 1, "S"), ("C1", 0, "G"), ("M1", 1, 1),
+    ("A1", 1, 0), ("EX", "a", 2, 0, "S"), ("Q", "z", 2), ("T", "w", 2, 0), ("A1", 1, 1), ("T", "w", 2, 1),
+    ("EX", "w", 2, 0, "S"), ("T", "w", 3, 0), ("NM1", 1), ("EX", "w", 2, 1, "V"), ("T", "w", 3, 1), ("B1", 1),
+    ("T", "z", 3, 0), ("Q", "w", 2), ("T", "z", 3, 1), ("T", "a", 3, 0), ("EX", "w", 3, 1, "V"), ("EX", "w", 3, 0, "S"),
+    ("R1", 1), ("Q", "a", 2), ("EX", "z", 3, 0, "S"), ("TP", 0, 0), ("Q", "w", 3), ("TP", 0, 1),
+    ("EX", "z", 3, 1, "S"), ("M1", 2, 0), ("C1", 1, "G"), ("EX", "a", 3, 0, "S"), ("Q", "z", 3), ("E1", 0, 0, "S"),
+    ("Q", "a", 3), ("M1", 2, 1), ("A1", 2, 0), ("E1", 0, 1, "S"), ("T", "w", 4, 0), ("A1", 2, 1),
+    ("T", "w", 4, 1), ("EX", "w", 4, 0, "S"), ("RG", 0, "V"), ("T", "w", 5, 0), ("T", "w", 5, 1), ("EX", "w", 5, 0, "S"),
+    ("T", "w", 6, 0), ("EX", "w", 4, 1, "V"), ("T", "w", 6, 1), ("EX", "w", 6, 0, "S"), ("EX", "w", 5, 1, "V"), ("T", "w", 7, 0),
+    ("T", "w", 7, 1), ("EX", "w", 7, 0, "S"), ("EX", "w", 6, 1, "V"), ("T", "z", 4, 0), ("T", "z", 4, 1), ("EX", "w", 7, 1, "V"),
+    ("T", "a", 4, 0), ("Q", "w", 4), ("TP", 1, 0), ("EX", "a", 4, 0, "S"), ("TP", 1, 1), ("Q", "w", 5),
+    ("E1", 1, 0, "S"), ("Q", "w", 6), ("E1", 1, 1, "S"), ("Q", "w", 7), ("EX", "z", 4, 0, "S"), ("QP", 0),
+    ("RG", 1, "V"), ("EX", "z", 4, 1, "S"), ("M2", 0, 0), ("QP", 1), ("NM1", 2), ("Q", "z", 4),
+    ("B1", 2), ("M2", 0, 1), ("A2", 0, 0), ("Q", "a", 4), ("R1", 2), ("M1", 3, 0),
+    ("A2", 0, 1), ("NM2", 0), ("C2", 0), ("B2", 0), ("M1", 3, 1), ("C1", 2, "G"),
+    ("A1", 3, 0), ("T", "z", 5, 0), ("R2", 0), ("A1", 3, 1), ("T", "z", 5, 1), ("EX", "z", 5, 0, "S"),
+    ("T", "a", 5, 0), ("NM1", 3), ("TP", 2, 0), ("EX", "z", 5, 1, "S"), ("TP", 2, 1), ("B1", 3),
+    ("D2", 0), ("M2", 1, 0), ("E1", 2, 0, "S"), ("Q", "z", 5), ("R1", 3), ("M2", 1, 1),
+    ("A2", 1, 0), ("E1", 2, 1, "S"), ("M1", 4, 0), ("C1", 3, "G"), ("A2", 1, 1), ("EX", "a", 5, 0, "S"),
+    ("RG", 2, "V"), ("E2", 0), ("M1", 4, 1), ("A1", 4, 0), ("ST", 0), ("QP", 2),
+    ("T", "z", 6, 0), ("A1", 4, 1), ("T", "z", 6, 1), ("EX", "z", 6, 0, "S"), ("T", "a", 6, 0), ("NM1", 4),
+    ("NM2", 1), ("C2", 1), ("TP", 3, 0), ("B1", 4), ("TP", 3, 1), ("M2", 2, 0),
+    ("Q", "a", 5), ("E1", 3, 0, "S"), ("R1", 4), ("M2", 2, 1), ("E1", 3, 1, "S"), ("A2", 2, 0),
+    ("C1", 4, "G"), ("B2", 1), ("RG", 3, "V"), ("M1", 5, 0), ("A2", 2, 1), ("EX", "z", 6, 1, "S"),
+    ("R2", 1), ("M1", 5, 1), ("QP", 3), ("EX", "a", 6, 0, "S"), ("A1", 5, 0), ("Q", "z", 6),
+    ("T", "z", 7, 0), ("A1", 5, 1), ("T", "z", 7, 1), ("EX", "z", 7, 0, "S"), ("T", "a", 7, 0), ("NM2", 2),
+    ("TP", 4, 0), ("EX", "z", 7, 1, "S"), ("C2", 2), ("TP", 4, 1), ("E1", 4, 0, "S"), ("M2", 3, 0),
+    ("Q", "z", 7), ("E1", 4, 1, "S"), ("NM1", 5), ("D2", 1), ("M2", 3, 1), ("B2", 2),
+    ("RG", 4, "V"), ("M1", 6, 0), ("B1", 5), ("R2", 2), ("A2", 3, 0), ("A2", 3, 1),
+    ("M1", 6, 1), ("EX", "a", 7, 0, "S"), ("R1", 5), ("QP", 4), ("E2", 1), ("A1", 6, 0),
+    ("A1", 6, 1), ("C1", 5, "G"), ("ST", 1), ("NM1", 6), ("D2", 2), ("B1", 6),
+    ("TP", 5, 0), ("NM2", 3), ("Q", "a", 6), ("E2", 2), ("TP", 5, 1), ("R1", 6),
+    ("C2", 3), ("M2", 4, 0), ("E1", 5, 0, "S"), ("ST", 2), ("Q", "a", 7), ("C1", 6, "G"),
+    ("M2", 4, 1), ("A2", 4, 0), ("E1", 5, 1, "S"), ("B2", 3), ("M1", 7, 0), ("RG", 5, "V"),
+    ("A2", 4, 1), ("M1", 7, 1), ("R2", 3), ("A1", 7, 0), ("NM2", 4), ("QP", 5),
+    ("TP", 6, 0), ("B2", 4), ("A1", 7, 1), ("TP", 6, 1), ("M2", 5, 0), ("NM1", 7),
+    ("C2", 4), ("B1", 7), ("R2", 4), ("M2", 5, 1), ("D2", 3), ("E1", 6, 0, "S"),
+    ("R1", 7), ("E1", 6, 1, "S"), ("A2", 5, 0), ("A2", 5, 1), ("C1", 7, "G"), ("E2", 3),
+    ("RG", 6, "V"), ("ST", 3), ("QP", 6), ("TP", 7, 0), ("NM2", 5), ("D2", 4),
+    ("B2", 5), ("TP", 7, 1), ("M2", 6, 0), ("C2", 5), ("E1", 7, 0, "S"), ("R2", 5),
+    ("M2", 6, 1), ("E1", 7, 1, "S"), ("A2", 6, 0), ("E2", 4), ("D2", 5), ("RG", 7, "V"),
+    ("ST", 4), ("E2", 5), ("QP", 7), ("A2", 6, 1), ("M2", 7, 0), ("ST", 5),
+    ("NM2", 6), ("C2", 6), ("B2", 6), ("M2", 7, 1), ("A2", 7, 0), ("R2", 6),
+    ("A2", 7, 1), ("NM2", 7), ("C2", 7), ("B2", 7), ("D2", 6), ("R2", 7),
+    ("E2", 6), ("D2", 7), ("ST", 6), ("E2", 7), ("ST", 7),
+)
 
 
 def tile_synapsemodel_pa_kernel(tc, z, attention_out, Wz, bz, gz, bz_ln, w1_deq, b1, g1, b1_ln, out):
@@ -31,14 +96,15 @@ def tile_synapsemodel_pa_kernel(tc, z, attention_out, Wz, bz, gz, bz_ln, w1_deq,
         rawa = ctx.enter_context(tc.tile_pool(name="rawa", bufs=4))
         stage = ctx.enter_context(tc.tile_pool(name="stage", bufs=4))
         stagea = ctx.enter_context(tc.tile_pool(name="stagea", bufs=3))
-        rows1 = ctx.enter_context(tc.tile_pool(name="rows1", bufs=6))
+        rows1 = ctx.enter_context(tc.tile_pool(name="rows1", bufs=4))
         rows2 = ctx.enter_context(tc.tile_pool(name="rows2", bufs=2))
         rows3 = ctx.enter_context(tc.tile_pool(name="rows3", bufs=3))
         junkp = ctx.enter_context(tc.tile_pool(name="junkp", bufs=2))
         plan = ctx.enter_context(tc.tile_pool(name="plan", bufs=2))
-        small = ctx.enter_context(tc.tile_pool(name="small", bufs=4))
-        ps_t = ctx.enter_context(tc.psum_pool(name="ps_t", bufs=4))
-        ps_a = ctx.enter_context(tc.psum_pool(name="ps_a", bufs=4))
+        small = ctx.enter_context(tc.tile_pool(name="small", bufs=6))
+        ps_t = ctx.enter_context(tc.psum_pool(name="ps_t", bufs=5))
+        ps_a = ctx.enter_context(tc.psum_pool(name="ps_a", bufs=3))
+        ctx.enter_context(tc.manual_schedule())
 
         ident = const.tile([P, P], F32, name="ident")
         make_identity(nc, ident[:])
@@ -46,7 +112,6 @@ def tile_synapsemodel_pa_kernel(tc, z, attention_out, Wz, bz, gz, bz_ln, w1_deq,
         nc.vector.tensor_copy(out=identb[:], in_=ident[:])
         mhalf = const.tile([P, 1], F32, name="mhalf")
         nc.vector.memset(mhalf[:], -0.5)
-
         vrows1 = const.tile([P, 512], BF16, name="vrows1")
         nc.vector.memset(vrows1[:].bitcast(I32), 0)
         grows = const.tile([P, 256], BF16, name="grows")
@@ -56,31 +121,11 @@ def tile_synapsemodel_pa_kernel(tc, z, attention_out, Wz, bz, gz, bz_ln, w1_deq,
         nc.scalar.dma_start(out=vrows1[0:2, :], in_=bz.rearrange("(a c) -> a c", a=2))
         nc.scalar.dma_start(out=grows[0:4, :], in_=gz.rearrange("(a c) -> a c", a=4))
         nc.scalar.dma_start(out=grows[4:8, :], in_=bz_ln.rearrange("(a c) -> a c", a=4))
-        nc.gpsimd.dma_start(out=vrows2[2:4, :], in_=b1.rearrange("(a c) -> a c", a=2))
-        nc.gpsimd.dma_start(out=vrows2[4:6, :], in_=g1.rearrange("(a c) -> a c", a=2))
-        nc.gpsimd.dma_start(out=vrows2[6:8, :], in_=b1_ln.rearrange("(a c) -> a c", a=2))
+        nc.scalar.dma_start(out=vrows2[2:4, :], in_=b1.rearrange("(a c) -> a c", a=2))
+        nc.scalar.dma_start(out=vrows2[4:6, :], in_=g1.rearrange("(a c) -> a c", a=2))
+        nc.scalar.dma_start(out=vrows2[6:8, :], in_=b1_ln.rearrange("(a c) -> a c", a=2))
 
         wz_v = Wz.rearrange("(a q e) k -> a e q k", q=P, e=2)
-        order = (
-            [("W", j) for j in range(4)] + [("z", 0), ("z", 1)] + [("W", j) for j in range(4, 8)]
-            + [("z", 2), ("z", 3)] + [("w", j) for j in range(8)] + [("a", i) for i in range(4)]
-            + [("z", i) for i in range(4, 8)] + [("a", i) for i in range(4, 8)]
-        )
-        loaded = {}
-        for kind, idx in order:
-            if kind == "a":
-                t = rawa.tile([P, H], BF16, tag="rawa")
-                src = attention_out[idx * P:(idx + 1) * P, :]
-            else:
-                t = raw.tile([P, D_IN], BF16, tag="raw")
-                if kind == "W":
-                    src = wz_v[idx // 2, idx % 2]
-                elif kind == "z":
-                    src = z[idx * P:(idx + 1) * P, :]
-                else:
-                    src = w1_deq[idx * P:(idx + 1) * P, :]
-            nc.sync.dma_start(out=t[:], in_=src)
-            loaded[(kind, idx)] = t
 
         zq = keep.tile([P, 8 * 512], U32, name="zq", align_bytes=64)
         zs = keep.tile([P, 8 * 512], U8, name="zs", align_bytes=64)
@@ -88,25 +133,21 @@ def tile_synapsemodel_pa_kernel(tc, z, attention_out, Wz, bz, gz, bz_ln, w1_deq,
         ws = keep.tile([P, 4 * 1024], U8, name="ws", align_bytes=64)
         vq = keep.tile([P, 4 * 1024], U32, name="vq", align_bytes=64)
         vs = keep.tile([P, 4 * 1024], U8, name="vs", align_bytes=64)
-        pq = keep.tile([P, 4 * 512], U32, name="pq", align_bytes=64)
-        pscl = keep.tile([P, 4 * 512], U8, name="pscl", align_bytes=64)
+        pq = keep.tile([P, 8 * 256], U32, name="pq", align_bytes=64)
+        pscl = keep.tile([P, 8 * 256], U8, name="pscl", align_bytes=64)
         aq = keep.tile([P, 8 * 256], U32, name="aq", align_bytes=64)
         ascl = keep.tile([P, 8 * 256], U8, name="ascl", align_bytes=64)
-
         bc = const.tile([P, 4 * 1024], BF16, name="bc")
         gb = const.tile([P, 16], F32, name="gb")
-        counter = [0]
 
-        def exit_copy(dst, src):
-            counter[0] += 1
-            if VEC_EXIT_EVERY and counter[0] % VEC_EXIT_EVERY == 0:
-                nc.vector.tensor_copy(out=dst, in_=src)
-            else:
-                nc.scalar.copy(out=dst, in_=src)
+        st = {}
 
         def bcast(r):
             pb = ps_t.tile([P, 512], F32, tag="tp")
-            nc.tensor.matmul(pb[:], lhsT=identb[:, r:r + 1].to_broadcast([P, P]), rhs=(vrows1 if r < 2 else vrows2)[:], start=True, stop=True)
+            nc.tensor.matmul(
+                pb[:], lhsT=identb[:, r:r + 1].to_broadcast([P, P]), rhs=(vrows1 if r < 2 else vrows2)[:],
+                start=True, stop=True,
+            )
             dst = bc[:, r * 512:(r + 1) * 512]
             if r < 2:
                 nc.vector.tensor_copy(
@@ -116,7 +157,7 @@ def tile_synapsemodel_pa_kernel(tc, z, attention_out, Wz, bz, gz, bz_ln, w1_deq,
             else:
                 nc.vector.tensor_copy(out=dst, in_=pb[:])
 
-        def consts_a():
+        def op_CA():
             bcast(0)
             bcast(1)
             g32 = const.tile([P, 256], F32, name="g32")
@@ -131,28 +172,46 @@ def tile_synapsemodel_pa_kernel(tc, z, attention_out, Wz, bz, gz, bz_ln, w1_deq,
                 in_=pg[:, 0:256].rearrange("p (e r) -> p e r", e=2)[:, :, 0:8].rearrange("p e (w a) -> p w a e", w=2),
             )
 
-        def consts_b():
-            for r in range(2, 8):
-                bcast(r)
-
-        def do_input(kind, idx):
-            t = loaded[(kind, idx)]
-            width = H if kind == "a" else D_IN
-            words = t[:].bitcast(F32)
+        def op_LD(kind, idx):
             if kind == "a":
-                grouped = stagea.tile([P, width], BF16, tag="grpa", align_bytes=64)
+                t = rawa.tile([P, H], BF16, tag="rawa")
+                src = attention_out[idx * P:(idx + 1) * P, :]
             else:
-                grouped = stage.tile([P, width], BF16, tag="grp", align_bytes=64)
-            gw = grouped[:].bitcast(F32)
-            for b in range(width // 1024):
-                xt = ps_t.tile([P, 512], F32, tag="tp")
-                for s in range(4):
-                    c0 = (4 * b + s) * P
-                    nc.tensor.transpose(xt[:, s * P:(s + 1) * P], words[:, c0:c0 + P], ident[:])
-                exit_copy(
-                    gw[:, b * 512:(b + 1) * 512].rearrange("p (g r u) -> p g r u", g=2, u=2),
-                    xt[:].rearrange("p (g u r) -> p g r u", g=2, u=2),
-                )
+                t = raw.tile([P, D_IN], BF16, tag="raw")
+                if kind == "W":
+                    src = wz_v[idx // 2, idx % 2]
+                elif kind == "z":
+                    src = z[idx * P:(idx + 1) * P, :]
+                else:
+                    src = w1_deq[idx * P:(idx + 1) * P, :]
+            nc.sync.dma_start(out=t[:], in_=src)
+            st[("raw", kind, idx)] = t
+
+        def op_T(kind, idx, b):
+            words = st[("raw", kind, idx)][:].bitcast(F32)
+            xt = ps_t.tile([P, 512], F32, tag="tp")
+            for s in range(4):
+                c0 = (4 * b + s) * P
+                nc.tensor.transpose(xt[:, s * P:(s + 1) * P], words[:, c0:c0 + P], ident[:])
+            st[("xt", kind, idx, b)] = xt
+
+        def op_EX(kind, idx, b, eng):
+            if ("grp", kind, idx) not in st:
+                if kind == "a":
+                    grouped = stagea.tile([P, H], BF16, tag="grpa", align_bytes=64)
+                else:
+                    grouped = stage.tile([P, D_IN], BF16, tag="grp", align_bytes=64)
+                st[("grp", kind, idx)] = grouped
+            gw = st[("grp", kind, idx)][:].bitcast(F32)
+            dst = gw[:, b * 512:(b + 1) * 512].rearrange("p (g r u) -> p g r u", g=2, u=2)
+            src = st[("xt", kind, idx, b)][:].rearrange("p (g u r) -> p g r u", g=2, u=2)
+            if eng == "V":
+                nc.vector.tensor_copy(out=dst, in_=src)
+            else:
+                nc.scalar.copy(out=dst, in_=src)
+
+        def op_Q(kind, idx):
+            grouped = st[("grp", kind, idx)]
             if kind == "z":
                 sl = slice(idx * 512, (idx + 1) * 512)
                 nc.vector.quantize_mx(out=zq[:, sl].bitcast(FP8X4), scales=zs[:, sl], in_=grouped[:])
@@ -167,146 +226,181 @@ def tile_synapsemodel_pa_kernel(tc, z, attention_out, Wz, bz, gz, bz_ln, w1_deq,
                         out=cq[:, sl].bitcast(FP8X4), scales=cs[:, sl], in_=grouped[:, g * 512:(g + 1) * 512]
                     )
 
-        def stats_tail(y, s):
+        def op_M(stg, i, n):
+            acc = ps_a.tile([P, 512], F32, tag="acc")
+            for g in range(4):
+                if stg == 1:
+                    c0 = i * 512 + g * P
+                    lq, ls, rq, rs = zq, zs, wq, ws
+                else:
+                    c0 = i * 256 + (g % 2) * P
+                    lq, ls = (pq, pscl) if g < 2 else (aq, ascl)
+                    rq, rs = vq, vs
+                sl = slice(c0, c0 + P)
+                sr = slice(g * 1024 + n * 512, g * 1024 + (n + 1) * 512)
+                nc.tensor.matmul_mx(
+                    out=acc[:], lhsT=lq[:, sl].bitcast(FP8X4), lhsT_scale=ls[:, sl],
+                    rhs=rq[:, sr].bitcast(FP8X4), rhs_scale=rs[:, sr], start=(g == 0), stop=(g == 3),
+                )
+            st[("acc", stg, i, n)] = acc
+
+        def op_A(stg, i, n):
+            if ("y", stg, i) not in st:
+                if stg == 1:
+                    y = rows1.tile([P, H], F32, tag="y1")
+                else:
+                    y = rows2.tile([P, H], F32, tag="y2")
+                s = small.tile([P, 2], F32, tag="s")
+                st[("y", stg, i)] = y
+                st[("s", stg, i)] = s
+            off = (stg - 1) * 1024 + n * 512
+            nc.vector.scalar_tensor_tensor(
+                out=st[("y", stg, i)][:, n * 512:(n + 1) * 512], in0=st[("acc", stg, i, n)][:], scalar=1.0,
+                in1=bc[:, off:off + 512], op0=ALU.mult, op1=ALU.add, accum_out=st[("s", stg, i)][:, n:n + 1],
+            )
+
+        def op_NM(stg, i):
+            s = st[("s", stg, i)]
             nm = small.tile([P, 1], F32, tag="nm")
             nc.vector.tensor_scalar(
                 out=nm[:], in0=s[:, 0:1], scalar1=s[:, 1:2], scalar2=-1.0 / H, op0=ALU.add, op1=ALU.mult
             )
+            st[("nm", stg, i)] = nm
+
+        def op_B(stg, i):
             junk = junkp.tile([P, H], BF16, tag="junk")
             ssq = small.tile([P, 1], F32, tag="ssq")
-            nc.scalar.activation(out=junk[:], in_=y[:], func=ACT.Square, bias=nm[:], scale=1.0, accum_out=ssq[:])
+            nc.scalar.activation(
+                out=junk[:], in_=st[("y", stg, i)][:], func=ACT.Square, bias=st[("nm", stg, i)][:], scale=1.0,
+                accum_out=ssq[:],
+            )
+            st[("ssq", stg, i)] = ssq
+
+        def op_R(stg, i):
             ve = small.tile([P, 1], F32, tag="ve")
-            nc.gpsimd.tensor_scalar(out=ve[:], in0=ssq[:], scalar1=1.0 / H, scalar2=LN_EPS, op0=ALU.mult, op1=ALU.add)
+            nc.gpsimd.tensor_scalar(
+                out=ve[:], in0=st[("ssq", stg, i)][:], scalar1=1.0 / H, scalar2=LN_EPS, op0=ALU.mult, op1=ALU.add
+            )
             rstd = small.tile([P, 1], F32, tag="rstd")
             nc.gpsimd.tensor_tensor(out=rstd[:], in0=ve[:], in1=mhalf[:], op=ALU.pow)
-            return nm, rstd
+            st[("rstd", stg, i)] = rstd
 
-        ys = {}
-        sums = {}
-
-        def m1(i, n):
-            acc = ps_a.tile([P, 512], F32, tag="acc")
-            for g in range(4):
-                sl = slice(i * 512 + g * P, i * 512 + (g + 1) * P)
-                sr = slice(g * 1024 + n * 512, g * 1024 + (n + 1) * 512)
-                nc.tensor.matmul_mx(
-                    out=acc[:], lhsT=zq[:, sl].bitcast(FP8X4), lhsT_scale=zs[:, sl],
-                    rhs=wq[:, sr].bitcast(FP8X4), rhs_scale=ws[:, sr], start=(g == 0), stop=(g == 3),
-                )
-            if n == 0:
-                y = rows1.tile([P, H], F32, tag="y1")
-                s = small.tile([P, 2], F32, tag="s")
-                ys[i] = y
-                sums[i] = s
-            nc.vector.scalar_tensor_tensor(
-                out=ys[i][:, n * 512:(n + 1) * 512], in0=acc[:], scalar=1.0, in1=bc[:, n * 512:(n + 1) * 512],
-                op0=ALU.mult, op1=ALU.add, accum_out=sums[i][:, n:n + 1],
+        def op_C1(i, eng):
+            y = st[("y", 1, i)]
+            e = nc.vector if eng == "V" else nc.gpsimd
+            e.tensor_scalar(
+                out=y[:], in0=y[:], scalar1=st[("nm", 1, i)][:], scalar2=st[("rstd", 1, i)][:],
+                op0=ALU.add, op1=ALU.mult,
             )
 
-        def ep1(i):
-            y = ys[i]
-            nm, rstd = stats_tail(y, sums[i])
-            nc.vector.tensor_scalar(out=y[:], in0=y[:], scalar1=nm[:], scalar2=rstd[:], op0=ALU.add, op1=ALU.mult)
+        def op_TP(i, g):
+            tp = ps_t.tile([P, 512], F32, tag="tp")
+            for t in range(4):
+                j = 4 * g + t
+                nc.tensor.transpose(tp[:, t * P:(t + 1) * P], st[("y", 1, i)][:, j * P:(j + 1) * P], ident[:])
+            st[("tp", i, g)] = tp
 
-        def tproj(b):
-            for g in range(2):
-                planar = plan.tile([P, 4 * 512], BF16, tag="planar")
-                for t in range(4):
-                    j = 4 * g + t
-                    tp = ps_t.tile([P, 512], F32, tag="tp")
-                    for c in range(4):
-                        nc.tensor.transpose(tp[:, c * P:(c + 1) * P], ys[4 * b + c][:, j * P:(j + 1) * P], ident[:])
+        def op_E1(i, g, eng):
+            if ("planar", i) not in st:
+                planar = plan.tile([P, H], BF16, tag="planar")
+                st[("planar", i)] = planar
+            for t in range(4):
+                j = 4 * g + t
+                dst = st[("planar", i)][:, j * P:(j + 1) * P]
+                src = st[("tp", i, g)][:, t * P:(t + 1) * P]
+                if eng == "V":
+                    nc.vector.tensor_scalar(
+                        out=dst, in0=src, scalar1=gb[:, j:j + 1], scalar2=gb[:, 8 + j:9 + j], op0=ALU.mult, op1=ALU.add
+                    )
+                else:
                     nc.scalar.activation(
-                        out=planar[:, t * 512:(t + 1) * 512], in_=tp[:], func=ACT.Identity,
-                        scale=gb[:, j:j + 1], bias=gb[:, 8 + j:9 + j],
+                        out=dst, in_=src, func=ACT.Identity, scale=gb[:, j:j + 1], bias=gb[:, 8 + j:9 + j]
                     )
-                gp = plan.tile([P, 4 * 512], BF16, tag="gp", align_bytes=64)
-                nc.vector.tensor_copy(
-                    out=gp[:].rearrange("p (c i t) -> p c t i", i=4, t=4),
-                    in_=planar[:].rearrange("p (t c i) -> p c t i", t=4, i=4),
-                )
-                sl = slice((2 * b + g) * 512, (2 * b + g + 1) * 512)
-                nc.vector.quantize_mx(out=pq[:, sl].bitcast(FP8X4), scales=pscl[:, sl], in_=gp[:])
 
-        def m2(i):
-            y = rows2.tile([P, H], F32, tag="y2")
-            s = small.tile([P, 2], F32, tag="s")
-            for n in range(2):
-                acc = ps_a.tile([P, 512], F32, tag="acc")
-                for g in range(4):
-                    if g < 2:
-                        c0 = (2 * (i // 4) + g) * 512 + (i % 4) * P
-                        lq, ls = pq, pscl
-                    else:
-                        c0 = i * 256 + (g - 2) * P
-                        lq, ls = aq, ascl
-                    sl = slice(c0, c0 + P)
-                    sr = slice(g * 1024 + n * 512, g * 1024 + (n + 1) * 512)
-                    nc.tensor.matmul_mx(
-                        out=acc[:], lhsT=lq[:, sl].bitcast(FP8X4), lhsT_scale=ls[:, sl],
-                        rhs=vq[:, sr].bitcast(FP8X4), rhs_scale=vs[:, sr], start=(g == 0), stop=(g == 3),
-                    )
-                nc.vector.scalar_tensor_tensor(
-                    out=y[:, n * 512:(n + 1) * 512], in0=acc[:], scalar=1.0,
-                    in1=bc[:, 1024 + n * 512:1024 + (n + 1) * 512],
-                    op0=ALU.mult, op1=ALU.add, accum_out=s[:, n:n + 1],
-                )
-            nm, rstd = stats_tail(y, s)
+        def op_RG(i, eng):
+            gp = plan.tile([P, H], BF16, tag="gp", align_bytes=64)
+            nc.vector.tensor_copy(
+                out=gp[:].rearrange("p (g c t) -> p g c t", g=2, t=4),
+                in_=st[("planar", i)][:].rearrange("p (g t c) -> p g c t", g=2, t=4),
+            )
+            st[("gp", i)] = gp
+
+        def op_QP(i):
+            sl = slice(i * 256, (i + 1) * 256)
+            nc.vector.quantize_mx(out=pq[:, sl].bitcast(FP8X4), scales=pscl[:, sl], in_=st[("gp", i)][:])
+
+        def op_C2(i):
             t2 = rows3.tile([P, H], F32, tag="t2")
             nc.vector.scalar_tensor_tensor(
-                out=t2[:], in0=y[:], scalar=nm[:], in1=bc[:, 2048:3072], op0=ALU.add, op1=ALU.mult
+                out=t2[:], in0=st[("y", 2, i)][:], scalar=st[("nm", 2, i)][:], in1=bc[:, 2048:3072],
+                op0=ALU.add, op1=ALU.mult,
             )
-            nc.vector.scalar_tensor_tensor(
-                out=t2[:], in0=t2[:], scalar=rstd[:], in1=bc[:, 3072:4096], op0=ALU.mult, op1=ALU.add
-            )
-            nc.scalar.activation(out=t2[:], in_=t2[:], func=ACT.Gelu)
-            nc.sync.dma_start(out=out[i * P:(i + 1) * P, :], in_=t2[:])
+            st[("t2", i)] = t2
 
-        for j in range(4):
-            do_input("W", j)
-        do_input("z", 0)
-        do_input("z", 1)
-        consts_a()
-        m1(0, 0)
-        m1(1, 0)
-        for j in range(4, 8):
-            do_input("W", j)
-        m1(0, 1)
-        ep1(0)
-        m1(1, 1)
-        ep1(1)
-        consts_b()
-        do_input("z", 2)
-        do_input("z", 3)
-        for i in (2, 3):
-            m1(i, 0)
-            m1(i, 1)
-            ep1(i)
-        for j in range(4):
-            do_input("w", j)
-        tproj(0)
-        for j in range(4, 8):
-            do_input("w", j)
-        for i in range(4):
-            do_input("a", i)
-        for i in (4, 5):
-            do_input("z", i)
-        for i in (4, 5):
-            m1(i, 0)
-            m1(i, 1)
-            ep1(i)
-        for i in (6, 7):
-            do_input("z", i)
-        for i in (6, 7):
-            m1(i, 0)
-            m1(i, 1)
-            ep1(i)
-        m2(0)
-        m2(1)
-        for i in range(4, 8):
-            do_input("a", i)
-        tproj(1)
-        m2(2)
-        m2(3)
-        for i in range(4, 8):
-            m2(i)
+        def op_D2(i):
+            t2 = st[("t2", i)]
+            nc.vector.scalar_tensor_tensor(
+                out=t2[:], in0=t2[:], scalar=st[("rstd", 2, i)][:], in1=bc[:, 3072:4096], op0=ALU.mult, op1=ALU.add
+            )
+
+        def op_E2(i):
+            t2 = st[("t2", i)]
+            nc.scalar.activation(out=t2[:], in_=t2[:], func=ACT.Gelu)
+
+        def op_ST(i):
+            nc.sync.dma_start(out=out[i * P:(i + 1) * P, :], in_=st[("t2", i)][:])
+
+        for step in SCHEDULE:
+            k = step[0]
+            a = step[1:]
+            if k == "LD":
+                op_LD(*a)
+            elif k == "CA":
+                op_CA()
+            elif k == "CB":
+                bcast(*a)
+            elif k == "T":
+                op_T(*a)
+            elif k == "EX":
+                op_EX(*a)
+            elif k == "Q":
+                op_Q(*a)
+            elif k == "M1":
+                op_M(1, *a)
+            elif k == "M2":
+                op_M(2, *a)
+            elif k == "A1":
+                op_A(1, *a)
+            elif k == "A2":
+                op_A(2, *a)
+            elif k == "NM1":
+                op_NM(1, *a)
+            elif k == "NM2":
+                op_NM(2, *a)
+            elif k == "B1":
+                op_B(1, *a)
+            elif k == "B2":
+                op_B(2, *a)
+            elif k == "R1":
+                op_R(1, *a)
+            elif k == "R2":
+                op_R(2, *a)
+            elif k == "C1":
+                op_C1(*a)
+            elif k == "TP":
+                op_TP(*a)
+            elif k == "E1":
+                op_E1(*a)
+            elif k == "RG":
+                op_RG(*a)
+            elif k == "QP":
+                op_QP(*a)
+            elif k == "C2":
+                op_C2(*a)
+            elif k == "D2":
+                op_D2(*a)
+            elif k == "E2":
+                op_E2(*a)
+            else:
+                assert k == "ST"
+                op_ST(*a)

@@ -21,69 +21,69 @@ FLOPS = 2 * N_TOK * D_IN * H + 2 * N_TOK * (2 * H) * H
 
 SCHEDULE = (
     ("LD", "W", 0), ("LD", "W", 1), ("LD", "W", 2), ("LD", "W", 3), ("LD", "W", 4), ("LD", "W", 5),
-    ("LD", "W", 6), ("LD", "W", 7), ("LD", "z", 0), ("LD", "a", 0), ("LD", "z", 1), ("LD", "a", 1),
-    ("LD", "w", 0), ("LD", "w", 1), ("LD", "z", 2), ("LD", "a", 2), ("LD", "w", 2), ("LD", "w", 3),
-    ("LD", "z", 3), ("LD", "a", 3), ("LD", "w", 4), ("LD", "w", 5), ("LD", "w", 6), ("LD", "w", 7),
-    ("LD", "z", 4), ("LD", "a", 4), ("LD", "z", 5), ("LD", "a", 5), ("LD", "z", 6), ("LD", "a", 6),
-    ("LD", "z", 7), ("LD", "a", 7), ("CA",), ("T", "W", 0, 0), ("T", "W", 0, 1), ("EX", "W", 0, 0, "S"),
-    ("EX", "W", 0, 1, "V"), ("T", "W", 1, 0), ("Q", "W", 0), ("T", "W", 1, 1), ("CB", 2), ("EX", "W", 1, 0, "S"),
-    ("EX", "W", 1, 1, "V"), ("T", "W", 2, 0), ("Q", "W", 1), ("T", "W", 2, 1), ("CB", 3), ("EX", "W", 2, 0, "S"),
-    ("EX", "W", 2, 1, "V"), ("T", "W", 3, 0), ("T", "W", 3, 1), ("CB", 4), ("Q", "W", 2), ("EX", "W", 3, 0, "S"),
-    ("EX", "W", 3, 1, "V"), ("T", "W", 4, 0), ("T", "W", 4, 1), ("CB", 5), ("EX", "W", 4, 0, "S"), ("Q", "W", 3),
-    ("T", "W", 5, 0), ("EX", "W", 4, 1, "V"), ("T", "W", 5, 1), ("CB", 6), ("EX", "W", 5, 0, "S"), ("Q", "W", 4),
-    ("T", "W", 6, 0), ("EX", "W", 5, 1, "V"), ("T", "W", 6, 1), ("CB", 7), ("EX", "W", 6, 0, "S"), ("Q", "W", 5),
-    ("T", "W", 7, 0), ("EX", "W", 6, 1, "V"), ("T", "W", 7, 1), ("EX", "W", 7, 0, "S"), ("Q", "W", 6), ("T", "z", 0, 0),
-    ("EX", "W", 7, 1, "V"), ("T", "z", 0, 1), ("EX", "z", 0, 0, "S"), ("T", "a", 0, 0), ("Q", "W", 7), ("EX", "z", 0, 1, "S"),
-    ("EX", "a", 0, 0, "S"), ("Q", "z", 0), ("T", "z", 1, 0), ("T", "z", 1, 1), ("EX", "z", 1, 0, "S"), ("Q", "a", 0),
-    ("T", "a", 1, 0), ("M1", 0, 0), ("EX", "z", 1, 1, "S"), ("EX", "a", 1, 0, "S"), ("Q", "z", 1), ("M1", 0, 1),
-    ("Q", "a", 1), ("A1", 0, 0), ("T", "w", 0, 0), ("A1", 0, 1), ("T", "w", 0, 1), ("EX", "w", 0, 0, "S"),
-    ("NM1", 0), ("T", "w", 1, 0), ("EX", "w", 0, 1, "V"), ("T", "w", 1, 1), ("B1", 0), ("T", "z", 2, 0),
-    ("Q", "w", 0), ("T", "z", 2, 1), ("EX", "w", 1, 1, "V"), ("T", "a", 2, 0), ("EX", "w", 1, 0, "S"), ("R1", 0),
-    ("M1", 1, 0), ("EX", "z", 2, 0, "S"), ("Q", "w", 1), ("EX", "z", 2, 1, "S"), ("C1", 0, "G"), ("M1", 1, 1),
-    ("A1", 1, 0), ("EX", "a", 2, 0, "S"), ("Q", "z", 2), ("T", "w", 2, 0), ("A1", 1, 1), ("T", "w", 2, 1),
-    ("EX", "w", 2, 0, "S"), ("T", "w", 3, 0), ("NM1", 1), ("EX", "w", 2, 1, "V"), ("T", "w", 3, 1), ("B1", 1),
-    ("T", "z", 3, 0), ("Q", "w", 2), ("T", "z", 3, 1), ("T", "a", 3, 0), ("EX", "w", 3, 1, "V"), ("EX", "w", 3, 0, "S"),
-    ("R1", 1), ("Q", "a", 2), ("EX", "z", 3, 0, "S"), ("TP", 0, 0), ("Q", "w", 3), ("TP", 0, 1),
-    ("EX", "z", 3, 1, "S"), ("M1", 2, 0), ("C1", 1, "G"), ("EX", "a", 3, 0, "S"), ("Q", "z", 3), ("E1", 0, 0, "S"),
-    ("Q", "a", 3), ("M1", 2, 1), ("A1", 2, 0), ("E1", 0, 1, "S"), ("T", "w", 4, 0), ("A1", 2, 1),
-    ("T", "w", 4, 1), ("EX", "w", 4, 0, "S"), ("RG", 0, "V"), ("T", "w", 5, 0), ("T", "w", 5, 1), ("EX", "w", 5, 0, "S"),
-    ("T", "w", 6, 0), ("EX", "w", 4, 1, "V"), ("T", "w", 6, 1), ("EX", "w", 6, 0, "S"), ("EX", "w", 5, 1, "V"), ("T", "w", 7, 0),
-    ("T", "w", 7, 1), ("EX", "w", 7, 0, "S"), ("EX", "w", 6, 1, "V"), ("T", "z", 4, 0), ("T", "z", 4, 1), ("EX", "w", 7, 1, "V"),
-    ("T", "a", 4, 0), ("Q", "w", 4), ("TP", 1, 0), ("EX", "a", 4, 0, "S"), ("TP", 1, 1), ("Q", "w", 5),
-    ("E1", 1, 0, "S"), ("Q", "w", 6), ("E1", 1, 1, "S"), ("Q", "w", 7), ("EX", "z", 4, 0, "S"), ("QP", 0),
-    ("RG", 1, "V"), ("EX", "z", 4, 1, "S"), ("M2", 0, 0), ("QP", 1), ("NM1", 2), ("Q", "z", 4),
-    ("B1", 2), ("M2", 0, 1), ("A2", 0, 0), ("Q", "a", 4), ("R1", 2), ("M1", 3, 0),
-    ("A2", 0, 1), ("NM2", 0), ("C2", 0), ("B2", 0), ("M1", 3, 1), ("C1", 2, "G"),
-    ("A1", 3, 0), ("T", "z", 5, 0), ("R2", 0), ("A1", 3, 1), ("T", "z", 5, 1), ("EX", "z", 5, 0, "S"),
-    ("T", "a", 5, 0), ("NM1", 3), ("TP", 2, 0), ("EX", "z", 5, 1, "S"), ("TP", 2, 1), ("B1", 3),
-    ("D2", 0), ("M2", 1, 0), ("E1", 2, 0, "S"), ("Q", "z", 5), ("R1", 3), ("M2", 1, 1),
-    ("A2", 1, 0), ("E1", 2, 1, "S"), ("M1", 4, 0), ("C1", 3, "G"), ("A2", 1, 1), ("EX", "a", 5, 0, "S"),
-    ("RG", 2, "V"), ("E2", 0), ("M1", 4, 1), ("A1", 4, 0), ("ST", 0), ("QP", 2),
-    ("T", "z", 6, 0), ("A1", 4, 1), ("T", "z", 6, 1), ("EX", "z", 6, 0, "S"), ("T", "a", 6, 0), ("NM1", 4),
-    ("NM2", 1), ("C2", 1), ("TP", 3, 0), ("B1", 4), ("TP", 3, 1), ("M2", 2, 0),
-    ("Q", "a", 5), ("E1", 3, 0, "S"), ("R1", 4), ("M2", 2, 1), ("E1", 3, 1, "S"), ("A2", 2, 0),
-    ("C1", 4, "G"), ("B2", 1), ("RG", 3, "V"), ("M1", 5, 0), ("A2", 2, 1), ("EX", "z", 6, 1, "S"),
-    ("R2", 1), ("M1", 5, 1), ("QP", 3), ("EX", "a", 6, 0, "S"), ("A1", 5, 0), ("Q", "z", 6),
-    ("T", "z", 7, 0), ("A1", 5, 1), ("T", "z", 7, 1), ("EX", "z", 7, 0, "S"), ("T", "a", 7, 0), ("NM2", 2),
-    ("TP", 4, 0), ("EX", "z", 7, 1, "S"), ("C2", 2), ("TP", 4, 1), ("E1", 4, 0, "S"), ("M2", 3, 0),
-    ("Q", "z", 7), ("E1", 4, 1, "S"), ("NM1", 5), ("D2", 1), ("M2", 3, 1), ("B2", 2),
-    ("RG", 4, "V"), ("M1", 6, 0), ("B1", 5), ("R2", 2), ("A2", 3, 0), ("A2", 3, 1),
-    ("M1", 6, 1), ("EX", "a", 7, 0, "S"), ("R1", 5), ("QP", 4), ("E2", 1), ("A1", 6, 0),
-    ("A1", 6, 1), ("C1", 5, "G"), ("ST", 1), ("NM1", 6), ("D2", 2), ("B1", 6),
-    ("TP", 5, 0), ("NM2", 3), ("Q", "a", 6), ("E2", 2), ("TP", 5, 1), ("R1", 6),
-    ("C2", 3), ("M2", 4, 0), ("E1", 5, 0, "S"), ("ST", 2), ("Q", "a", 7), ("C1", 6, "G"),
-    ("M2", 4, 1), ("A2", 4, 0), ("E1", 5, 1, "S"), ("B2", 3), ("M1", 7, 0), ("RG", 5, "V"),
-    ("A2", 4, 1), ("M1", 7, 1), ("R2", 3), ("A1", 7, 0), ("NM2", 4), ("QP", 5),
-    ("TP", 6, 0), ("B2", 4), ("A1", 7, 1), ("TP", 6, 1), ("M2", 5, 0), ("NM1", 7),
-    ("C2", 4), ("B1", 7), ("R2", 4), ("M2", 5, 1), ("D2", 3), ("E1", 6, 0, "S"),
-    ("R1", 7), ("E1", 6, 1, "S"), ("A2", 5, 0), ("A2", 5, 1), ("C1", 7, "G"), ("E2", 3),
-    ("RG", 6, "V"), ("ST", 3), ("QP", 6), ("TP", 7, 0), ("NM2", 5), ("D2", 4),
-    ("B2", 5), ("TP", 7, 1), ("M2", 6, 0), ("C2", 5), ("E1", 7, 0, "S"), ("R2", 5),
-    ("M2", 6, 1), ("E1", 7, 1, "S"), ("A2", 6, 0), ("E2", 4), ("D2", 5), ("RG", 7, "V"),
-    ("ST", 4), ("E2", 5), ("QP", 7), ("A2", 6, 1), ("M2", 7, 0), ("ST", 5),
-    ("NM2", 6), ("C2", 6), ("B2", 6), ("M2", 7, 1), ("A2", 7, 0), ("R2", 6),
-    ("A2", 7, 1), ("NM2", 7), ("C2", 7), ("B2", 7), ("D2", 6), ("R2", 7),
-    ("E2", 6), ("D2", 7), ("ST", 6), ("E2", 7), ("ST", 7),
+    ("LD", "W", 6), ("LD", "W", 7), ("LD", "z", 0), ("LD", "w", 0), ("LD", "w", 1), ("LD", "z", 1),
+    ("LD", "w", 2), ("LD", "w", 3), ("LD", "z", 2), ("LD", "w", 4), ("LD", "w", 5), ("LD", "z", 3),
+    ("LD", "w", 6), ("LD", "a", 0), ("LD", "w", 7), ("LD", "z", 4), ("LD", "a", 1), ("LD", "z", 5),
+    ("LD", "a", 2), ("LD", "z", 6), ("LD", "a", 3), ("LD", "z", 7), ("LD", "a", 4), ("LD", "a", 5),
+    ("LD", "a", 6), ("LD", "a", 7), ("T", "W", 0, 0), ("T", "W", 0, 1), ("EX", "W", 0, 0, "S"), ("T", "W", 1, 0),
+    ("EX", "W", 0, 1, "V"), ("T", "W", 1, 1), ("CA",), ("Q", "W", 0), ("EX", "W", 1, 0, "S"), ("T", "W", 2, 0),
+    ("T", "W", 2, 1), ("CB", 2), ("EX", "W", 1, 1, "V"), ("EX", "W", 2, 0, "S"), ("Q", "W", 1), ("T", "W", 3, 0),
+    ("T", "W", 3, 1), ("CB", 3), ("EX", "W", 2, 1, "V"), ("EX", "W", 3, 0, "S"), ("Q", "W", 2), ("T", "W", 4, 0),
+    ("T", "W", 4, 1), ("CB", 4), ("EX", "W", 3, 1, "V"), ("EX", "W", 4, 0, "S"), ("T", "W", 5, 0), ("Q", "W", 3),
+    ("T", "W", 5, 1), ("CB", 5), ("EX", "W", 4, 1, "V"), ("EX", "W", 5, 0, "S"), ("T", "W", 6, 0), ("Q", "W", 4),
+    ("T", "W", 6, 1), ("CB", 6), ("EX", "W", 5, 1, "V"), ("EX", "W", 6, 0, "S"), ("T", "W", 7, 0), ("EX", "W", 6, 1, "V"),
+    ("T", "W", 7, 1), ("CB", 7), ("Q", "W", 5), ("EX", "W", 7, 0, "S"), ("T", "z", 0, 0), ("EX", "W", 7, 1, "V"),
+    ("T", "z", 0, 1), ("Q", "W", 6), ("EX", "z", 0, 0, "S"), ("T", "w", 0, 0), ("EX", "z", 0, 1, "S"), ("Q", "W", 7),
+    ("T", "w", 0, 1), ("EX", "w", 0, 0, "S"), ("T", "w", 1, 0), ("EX", "w", 0, 1, "V"), ("T", "w", 1, 1), ("Q", "z", 0),
+    ("EX", "w", 1, 0, "S"), ("T", "z", 1, 0), ("EX", "w", 1, 1, "V"), ("T", "z", 1, 1), ("Q", "w", 0), ("EX", "z", 1, 0, "S"),
+    ("T", "w", 2, 0), ("Q", "w", 1), ("EX", "z", 1, 1, "S"), ("T", "w", 2, 1), ("M1", 0, 0), ("EX", "w", 2, 0, "S"),
+    ("EX", "w", 2, 1, "V"), ("Q", "z", 1), ("T", "w", 3, 0), ("Q", "w", 2), ("T", "w", 3, 1), ("M1", 0, 1),
+    ("EX", "w", 3, 0, "S"), ("A1", 0, 0), ("EX", "w", 3, 1, "V"), ("T", "z", 2, 0), ("Q", "w", 3), ("T", "z", 2, 1),
+    ("A1", 0, 1), ("T", "w", 4, 0), ("EX", "z", 2, 0, "S"), ("T", "w", 4, 1), ("NM1", 0), ("EX", "z", 2, 1, "S"),
+    ("M1", 1, 0), ("B1", 0), ("EX", "w", 4, 1, "V"), ("Q", "z", 2), ("T", "w", 5, 0), ("EX", "w", 4, 0, "S"),
+    ("T", "w", 5, 1), ("A1", 1, 0), ("R1", 0), ("M1", 1, 1), ("EX", "w", 5, 0, "S"), ("EX", "w", 5, 1, "V"),
+    ("Q", "w", 4), ("T", "z", 3, 0), ("Q", "w", 5), ("T", "z", 3, 1), ("T", "w", 6, 0), ("EX", "z", 3, 0, "S"),
+    ("A1", 1, 1), ("T", "w", 6, 1), ("EX", "z", 3, 1, "S"), ("T", "a", 0, 0), ("NM1", 1), ("M1", 2, 0),
+    ("EX", "w", 6, 0, "S"), ("EX", "w", 6, 1, "V"), ("B1", 1), ("Q", "z", 3), ("T", "w", 7, 0), ("C1", 0, "V"),
+    ("T", "w", 7, 1), ("EX", "a", 0, 0, "S"), ("A1", 2, 0), ("M1", 2, 1), ("R1", 1), ("EX", "w", 7, 0, "S"),
+    ("Q", "w", 6), ("EX", "w", 7, 1, "V"), ("T", "z", 4, 0), ("Q", "w", 7), ("T", "z", 4, 1), ("T", "a", 1, 0),
+    ("A1", 2, 1), ("EX", "z", 4, 0, "S"), ("M1", 3, 0), ("NM1", 2), ("EX", "z", 4, 1, "S"), ("Q", "a", 0),
+    ("EX", "a", 1, 0, "S"), ("TP", 0, 0), ("Q", "z", 4), ("B1", 2), ("M1", 3, 1), ("A1", 3, 0),
+    ("E1", 0, 0, "S"), ("C1", 1, "V"), ("TP", 0, 1), ("R1", 2), ("Q", "a", 1), ("T", "z", 5, 0),
+    ("A1", 3, 1), ("T", "z", 5, 1), ("E1", 0, 1, "S"), ("NM1", 3), ("T", "a", 2, 0), ("M1", 4, 0),
+    ("EX", "z", 5, 0, "S"), ("RG", 0, "V"), ("EX", "z", 5, 1, "S"), ("TP", 1, 0), ("B1", 3), ("QP", 0),
+    ("M1", 4, 1), ("A1", 4, 0), ("Q", "z", 5), ("E1", 1, 0, "S"), ("R1", 3), ("C1", 2, "V"),
+    ("TP", 1, 1), ("EX", "a", 2, 0, "S"), ("M2", 0, 0), ("A1", 4, 1), ("E1", 1, 1, "S"), ("NM1", 4),
+    ("Q", "a", 2), ("T", "z", 6, 0), ("B1", 4), ("T", "z", 6, 1), ("A2", 0, 0), ("M2", 0, 1),
+    ("RG", 1, "V"), ("EX", "z", 6, 0, "S"), ("EX", "z", 6, 1, "S"), ("QP", 1), ("R1", 4), ("T", "a", 3, 0),
+    ("C1", 3, "V"), ("M1", 5, 0), ("A2", 0, 1), ("EX", "a", 3, 0, "S"), ("Q", "z", 6), ("TP", 2, 0),
+    ("NM2", 0), ("Q", "a", 3), ("M1", 5, 1), ("A1", 5, 0), ("B2", 0), ("C2", 0),
+    ("TP", 2, 1), ("E1", 2, 0, "S"), ("M2", 1, 0), ("A1", 5, 1), ("R2", 0), ("E1", 2, 1, "S"),
+    ("NM1", 5), ("C1", 4, "V"), ("T", "z", 7, 0), ("B1", 5), ("T", "z", 7, 1), ("A2", 1, 0),
+    ("M2", 1, 1), ("RG", 2, "V"), ("EX", "z", 7, 0, "S"), ("QP", 2), ("EX", "z", 7, 1, "S"), ("T", "a", 4, 0),
+    ("M1", 6, 0), ("A2", 1, 1), ("R1", 5), ("EX", "a", 4, 0, "S"), ("Q", "z", 7), ("NM2", 1),
+    ("TP", 3, 0), ("C2", 1), ("M1", 6, 1), ("B2", 1), ("A1", 6, 0), ("E1", 3, 0, "S"),
+    ("TP", 3, 1), ("Q", "a", 4), ("D2", 0), ("M2", 2, 0), ("E1", 3, 1, "S"), ("R2", 1),
+    ("A1", 6, 1), ("M2", 2, 1), ("E2", 0), ("NM1", 6), ("C1", 5, "V"), ("A2", 2, 0),
+    ("T", "a", 5, 0), ("B1", 6), ("RG", 3, "V"), ("M1", 7, 0), ("ST", 0), ("A2", 2, 1),
+    ("EX", "a", 5, 0, "S"), ("TP", 4, 0), ("QP", 3), ("R1", 6), ("NM2", 2), ("C2", 2),
+    ("M1", 7, 1), ("B2", 2), ("A1", 7, 0), ("TP", 4, 1), ("E1", 4, 0, "S"), ("Q", "a", 5),
+    ("M2", 3, 0), ("A1", 7, 1), ("E1", 4, 1, "S"), ("NM1", 7), ("D2", 1), ("M2", 3, 1),
+    ("B1", 7), ("R2", 2), ("RG", 4, "V"), ("T", "a", 6, 0), ("E2", 1), ("C1", 6, "V"),
+    ("TP", 5, 0), ("TP", 5, 1), ("A2", 3, 0), ("EX", "a", 6, 0, "S"), ("QP", 4), ("ST", 1),
+    ("A2", 3, 1), ("E1", 5, 0, "S"), ("M2", 4, 0), ("NM2", 3), ("Q", "a", 6), ("E1", 5, 1, "S"),
+    ("C2", 3), ("R1", 7), ("B2", 3), ("M2", 4, 1), ("RG", 5, "V"), ("A2", 4, 0),
+    ("T", "a", 7, 0), ("TP", 6, 0), ("A2", 4, 1), ("TP", 6, 1), ("EX", "a", 7, 0, "S"), ("QP", 5),
+    ("NM2", 4), ("C2", 4), ("E1", 6, 0, "S"), ("M2", 5, 0), ("R2", 3), ("E1", 6, 1, "S"),
+    ("Q", "a", 7), ("C1", 7, "V"), ("B2", 4), ("M2", 5, 1), ("D2", 2), ("TP", 7, 0),
+    ("RG", 6, "V"), ("TP", 7, 1), ("E2", 2), ("QP", 6), ("A2", 5, 0), ("R2", 4),
+    ("M2", 6, 0), ("E1", 7, 0, "S"), ("A2", 5, 1), ("ST", 2), ("NM2", 5), ("D2", 3),
+    ("E1", 7, 1, "S"), ("M2", 6, 1), ("B2", 5), ("A2", 6, 0), ("RG", 7, "V"), ("E2", 3),
+    ("QP", 7), ("A2", 6, 1), ("R2", 5), ("M2", 7, 0), ("NM2", 6), ("C2", 5),
+    ("ST", 3), ("B2", 6), ("M2", 7, 1), ("C2", 6), ("A2", 7, 0), ("A2", 7, 1),
+    ("R2", 6), ("NM2", 7), ("C2", 7), ("B2", 7), ("D2", 4), ("D2", 5),
+    ("E2", 4), ("R2", 7), ("E2", 5), ("D2", 6), ("ST", 4), ("ST", 5),
+    ("E2", 6), ("ST", 6), ("D2", 7), ("E2", 7), ("ST", 7),
 )
 
 
@@ -97,11 +97,11 @@ def tile_synapsemodel_pa_kernel(tc, z, attention_out, Wz, bz, gz, bz_ln, w1_deq,
         stage = ctx.enter_context(tc.tile_pool(name="stage", bufs=4))
         stagea = ctx.enter_context(tc.tile_pool(name="stagea", bufs=3))
         rows1 = ctx.enter_context(tc.tile_pool(name="rows1", bufs=4))
-        rows2 = ctx.enter_context(tc.tile_pool(name="rows2", bufs=2))
-        rows3 = ctx.enter_context(tc.tile_pool(name="rows3", bufs=3))
+        rows2 = ctx.enter_context(tc.tile_pool(name="rows2", bufs=3))
+        rows3 = ctx.enter_context(tc.tile_pool(name="rows3", bufs=4))
         junkp = ctx.enter_context(tc.tile_pool(name="junkp", bufs=2))
         plan = ctx.enter_context(tc.tile_pool(name="plan", bufs=2))
-        small = ctx.enter_context(tc.tile_pool(name="small", bufs=6))
+        small = ctx.enter_context(tc.tile_pool(name="small", bufs=8))
         ps_t = ctx.enter_context(tc.psum_pool(name="ps_t", bufs=5))
         ps_a = ctx.enter_context(tc.psum_pool(name="ps_a", bufs=3))
         ctx.enter_context(tc.manual_schedule())
@@ -118,9 +118,9 @@ def tile_synapsemodel_pa_kernel(tc, z, attention_out, Wz, bz, gz, bz_ln, w1_deq,
         nc.vector.memset(grows[:].bitcast(I32), 0)
         vrows2 = const.tile([P, 512], BF16, name="vrows2")
         nc.vector.memset(vrows2[:].bitcast(I32), 0)
-        nc.scalar.dma_start(out=vrows1[0:2, :], in_=bz.rearrange("(a c) -> a c", a=2))
-        nc.scalar.dma_start(out=grows[0:4, :], in_=gz.rearrange("(a c) -> a c", a=4))
-        nc.scalar.dma_start(out=grows[4:8, :], in_=bz_ln.rearrange("(a c) -> a c", a=4))
+        nc.sync.dma_start(out=vrows1[0:2, :], in_=bz.rearrange("(a c) -> a c", a=2))
+        nc.sync.dma_start(out=grows[0:4, :], in_=gz.rearrange("(a c) -> a c", a=4))
+        nc.sync.dma_start(out=grows[4:8, :], in_=bz_ln.rearrange("(a c) -> a c", a=4))
         nc.scalar.dma_start(out=vrows2[2:4, :], in_=b1.rearrange("(a c) -> a c", a=2))
         nc.scalar.dma_start(out=vrows2[4:6, :], in_=g1.rearrange("(a c) -> a c", a=2))
         nc.scalar.dma_start(out=vrows2[6:8, :], in_=b1_ln.rearrange("(a c) -> a c", a=2))

@@ -16,75 +16,17 @@ P = 128
 N_TOK = 1024
 D_IN = 2048
 H = 1024
+BANK = 512
+PASSES = D_IN // 512
+TILES = N_TOK // P
 LN_EPS = 1e-5
-FLOPS = 2 * N_TOK * D_IN * H + 2 * N_TOK * (2 * H) * H
+FLOPS = 2 * N_TOK * D_IN * H + 2 * N_TOK * D_IN * H
 
-SCHEDULE = (
-    ("LD", "W", 0), ("LD", "W", 1), ("LD", "W", 2), ("LD", "W", 3), ("LD", "W", 4), ("LD", "W", 5),
-    ("LD", "W", 6), ("LD", "W", 7), ("LD", "z", 0), ("LD", "w", 0), ("LD", "w", 1), ("LD", "z", 1),
-    ("LD", "w", 2), ("LD", "w", 3), ("LD", "z", 2), ("LD", "w", 4), ("LD", "w", 5), ("LD", "z", 3),
-    ("LD", "w", 6), ("LD", "a", 0), ("LD", "w", 7), ("LD", "z", 4), ("LD", "a", 1), ("LD", "z", 5),
-    ("LD", "a", 2), ("LD", "z", 6), ("LD", "a", 3), ("LD", "z", 7), ("LD", "a", 4), ("LD", "a", 5),
-    ("LD", "a", 6), ("LD", "a", 7), ("T", "W", 0, 0), ("T", "W", 0, 1), ("EX", "W", 0, 0, "S"), ("T", "W", 1, 0),
-    ("EX", "W", 0, 1, "V"), ("T", "W", 1, 1), ("CA",), ("Q", "W", 0), ("EX", "W", 1, 0, "S"), ("T", "W", 2, 0),
-    ("T", "W", 2, 1), ("CB", 2), ("EX", "W", 1, 1, "V"), ("EX", "W", 2, 0, "S"), ("Q", "W", 1), ("T", "W", 3, 0),
-    ("T", "W", 3, 1), ("CB", 3), ("EX", "W", 2, 1, "V"), ("EX", "W", 3, 0, "S"), ("Q", "W", 2), ("T", "W", 4, 0),
-    ("T", "W", 4, 1), ("CB", 4), ("EX", "W", 3, 1, "V"), ("EX", "W", 4, 0, "S"), ("T", "W", 5, 0), ("Q", "W", 3),
-    ("T", "W", 5, 1), ("CB", 5), ("EX", "W", 4, 1, "V"), ("EX", "W", 5, 0, "S"), ("T", "W", 6, 0), ("Q", "W", 4),
-    ("T", "W", 6, 1), ("CB", 6), ("EX", "W", 5, 1, "V"), ("EX", "W", 6, 0, "S"), ("T", "W", 7, 0), ("EX", "W", 6, 1, "V"),
-    ("T", "W", 7, 1), ("CB", 7), ("Q", "W", 5), ("EX", "W", 7, 0, "S"), ("T", "z", 0, 0), ("EX", "W", 7, 1, "V"),
-    ("T", "z", 0, 1), ("Q", "W", 6), ("EX", "z", 0, 0, "S"), ("T", "w", 0, 0), ("EX", "z", 0, 1, "S"), ("Q", "W", 7),
-    ("T", "w", 0, 1), ("EX", "w", 0, 0, "S"), ("T", "w", 1, 0), ("EX", "w", 0, 1, "V"), ("T", "w", 1, 1), ("Q", "z", 0),
-    ("EX", "w", 1, 0, "S"), ("T", "z", 1, 0), ("EX", "w", 1, 1, "V"), ("T", "z", 1, 1), ("Q", "w", 0), ("EX", "z", 1, 0, "S"),
-    ("T", "w", 2, 0), ("Q", "w", 1), ("EX", "z", 1, 1, "S"), ("T", "w", 2, 1), ("M1", 0, 0), ("EX", "w", 2, 0, "S"),
-    ("EX", "w", 2, 1, "V"), ("Q", "z", 1), ("T", "w", 3, 0), ("Q", "w", 2), ("T", "w", 3, 1), ("M1", 0, 1),
-    ("EX", "w", 3, 0, "S"), ("A1", 0, 0), ("EX", "w", 3, 1, "V"), ("T", "z", 2, 0), ("Q", "w", 3), ("T", "z", 2, 1),
-    ("A1", 0, 1), ("T", "w", 4, 0), ("EX", "z", 2, 0, "S"), ("T", "w", 4, 1), ("NM1", 0), ("EX", "z", 2, 1, "S"),
-    ("M1", 1, 0), ("B1", 0), ("EX", "w", 4, 1, "V"), ("Q", "z", 2), ("T", "w", 5, 0), ("EX", "w", 4, 0, "S"),
-    ("T", "w", 5, 1), ("A1", 1, 0), ("R1", 0), ("M1", 1, 1), ("EX", "w", 5, 0, "S"), ("EX", "w", 5, 1, "V"),
-    ("Q", "w", 4), ("T", "z", 3, 0), ("Q", "w", 5), ("T", "z", 3, 1), ("T", "w", 6, 0), ("EX", "z", 3, 0, "S"),
-    ("A1", 1, 1), ("T", "w", 6, 1), ("EX", "z", 3, 1, "S"), ("T", "a", 0, 0), ("NM1", 1), ("M1", 2, 0),
-    ("EX", "w", 6, 0, "S"), ("EX", "w", 6, 1, "V"), ("B1", 1), ("Q", "z", 3), ("T", "w", 7, 0), ("C1", 0, "V"),
-    ("T", "w", 7, 1), ("EX", "a", 0, 0, "S"), ("A1", 2, 0), ("M1", 2, 1), ("R1", 1), ("EX", "w", 7, 0, "S"),
-    ("Q", "w", 6), ("EX", "w", 7, 1, "V"), ("T", "z", 4, 0), ("Q", "w", 7), ("T", "z", 4, 1), ("T", "a", 1, 0),
-    ("A1", 2, 1), ("EX", "z", 4, 0, "S"), ("M1", 3, 0), ("NM1", 2), ("EX", "z", 4, 1, "S"), ("Q", "a", 0),
-    ("EX", "a", 1, 0, "S"), ("TP", 0, 0), ("Q", "z", 4), ("B1", 2), ("M1", 3, 1), ("A1", 3, 0),
-    ("E1", 0, 0, "S"), ("C1", 1, "V"), ("TP", 0, 1), ("R1", 2), ("Q", "a", 1), ("T", "z", 5, 0),
-    ("A1", 3, 1), ("T", "z", 5, 1), ("E1", 0, 1, "S"), ("NM1", 3), ("T", "a", 2, 0), ("M1", 4, 0),
-    ("EX", "z", 5, 0, "S"), ("RG", 0, "V"), ("EX", "z", 5, 1, "S"), ("TP", 1, 0), ("B1", 3), ("QP", 0),
-    ("M1", 4, 1), ("A1", 4, 0), ("Q", "z", 5), ("E1", 1, 0, "S"), ("R1", 3), ("C1", 2, "V"),
-    ("TP", 1, 1), ("EX", "a", 2, 0, "S"), ("M2", 0, 0), ("A1", 4, 1), ("E1", 1, 1, "S"), ("NM1", 4),
-    ("Q", "a", 2), ("T", "z", 6, 0), ("B1", 4), ("T", "z", 6, 1), ("A2", 0, 0), ("M2", 0, 1),
-    ("RG", 1, "V"), ("EX", "z", 6, 0, "S"), ("EX", "z", 6, 1, "S"), ("QP", 1), ("R1", 4), ("T", "a", 3, 0),
-    ("C1", 3, "V"), ("M1", 5, 0), ("A2", 0, 1), ("EX", "a", 3, 0, "S"), ("Q", "z", 6), ("TP", 2, 0),
-    ("NM2", 0), ("Q", "a", 3), ("M1", 5, 1), ("A1", 5, 0), ("B2", 0), ("C2", 0),
-    ("TP", 2, 1), ("E1", 2, 0, "S"), ("M2", 1, 0), ("A1", 5, 1), ("R2", 0), ("E1", 2, 1, "S"),
-    ("NM1", 5), ("C1", 4, "V"), ("T", "z", 7, 0), ("B1", 5), ("T", "z", 7, 1), ("A2", 1, 0),
-    ("M2", 1, 1), ("RG", 2, "V"), ("EX", "z", 7, 0, "S"), ("QP", 2), ("EX", "z", 7, 1, "S"), ("T", "a", 4, 0),
-    ("M1", 6, 0), ("A2", 1, 1), ("R1", 5), ("EX", "a", 4, 0, "S"), ("Q", "z", 7), ("NM2", 1),
-    ("TP", 3, 0), ("C2", 1), ("M1", 6, 1), ("B2", 1), ("A1", 6, 0), ("E1", 3, 0, "S"),
-    ("TP", 3, 1), ("Q", "a", 4), ("D2", 0), ("M2", 2, 0), ("E1", 3, 1, "S"), ("R2", 1),
-    ("A1", 6, 1), ("M2", 2, 1), ("E2", 0), ("NM1", 6), ("C1", 5, "V"), ("A2", 2, 0),
-    ("T", "a", 5, 0), ("B1", 6), ("RG", 3, "V"), ("M1", 7, 0), ("ST", 0), ("A2", 2, 1),
-    ("EX", "a", 5, 0, "S"), ("TP", 4, 0), ("QP", 3), ("R1", 6), ("NM2", 2), ("C2", 2),
-    ("M1", 7, 1), ("B2", 2), ("A1", 7, 0), ("TP", 4, 1), ("E1", 4, 0, "S"), ("Q", "a", 5),
-    ("M2", 3, 0), ("A1", 7, 1), ("E1", 4, 1, "S"), ("NM1", 7), ("D2", 1), ("M2", 3, 1),
-    ("B1", 7), ("R2", 2), ("RG", 4, "V"), ("T", "a", 6, 0), ("E2", 1), ("C1", 6, "V"),
-    ("TP", 5, 0), ("TP", 5, 1), ("A2", 3, 0), ("EX", "a", 6, 0, "S"), ("QP", 4), ("ST", 1),
-    ("A2", 3, 1), ("E1", 5, 0, "S"), ("M2", 4, 0), ("NM2", 3), ("Q", "a", 6), ("E1", 5, 1, "S"),
-    ("C2", 3), ("R1", 7), ("B2", 3), ("M2", 4, 1), ("RG", 5, "V"), ("A2", 4, 0),
-    ("T", "a", 7, 0), ("TP", 6, 0), ("A2", 4, 1), ("TP", 6, 1), ("EX", "a", 7, 0, "S"), ("QP", 5),
-    ("NM2", 4), ("C2", 4), ("E1", 6, 0, "S"), ("M2", 5, 0), ("R2", 3), ("E1", 6, 1, "S"),
-    ("Q", "a", 7), ("C1", 7, "V"), ("B2", 4), ("M2", 5, 1), ("D2", 2), ("TP", 7, 0),
-    ("RG", 6, "V"), ("TP", 7, 1), ("E2", 2), ("QP", 6), ("A2", 5, 0), ("R2", 4),
-    ("M2", 6, 0), ("E1", 7, 0, "S"), ("A2", 5, 1), ("ST", 2), ("NM2", 5), ("D2", 3),
-    ("E1", 7, 1, "S"), ("M2", 6, 1), ("B2", 5), ("A2", 6, 0), ("RG", 7, "V"), ("E2", 3),
-    ("QP", 7), ("A2", 6, 1), ("R2", 5), ("M2", 7, 0), ("NM2", 6), ("C2", 5),
-    ("ST", 3), ("B2", 6), ("M2", 7, 1), ("C2", 6), ("A2", 7, 0), ("A2", 7, 1),
-    ("R2", 6), ("NM2", 7), ("C2", 7), ("B2", 7), ("D2", 4), ("D2", 5),
-    ("E2", 4), ("R2", 7), ("E2", 5), ("D2", 6), ("ST", 4), ("ST", 5),
-    ("E2", 6), ("ST", 6), ("D2", 7), ("E2", 7), ("ST", 7),
-)
+AHEAD_Z = 5
+AHEAD_M1 = 4
+AHEAD_A = 3
+AHEAD_ROWS = 2
+DRAIN_ROUNDS = 2
 
 
 def tile_synapsemodel_pa_kernel(tc, z, attention_out, Wz, bz, gz, bz_ln, w1_deq, b1, g1, b1_ln, out):
@@ -92,14 +34,14 @@ def tile_synapsemodel_pa_kernel(tc, z, attention_out, Wz, bz, gz, bz_ln, w1_deq,
     with ExitStack() as ctx:
         const = ctx.enter_context(tc.tile_pool(name="const", bufs=1))
         keep = ctx.enter_context(tc.tile_pool(name="keep", bufs=1))
-        raw = ctx.enter_context(tc.tile_pool(name="raw", bufs=10))
+        raw = ctx.enter_context(tc.tile_pool(name="raw", bufs=6))
         rawa = ctx.enter_context(tc.tile_pool(name="rawa", bufs=4))
-        stage = ctx.enter_context(tc.tile_pool(name="stage", bufs=4))
-        stagea = ctx.enter_context(tc.tile_pool(name="stagea", bufs=3))
+        stage = ctx.enter_context(tc.tile_pool(name="stage", bufs=3))
+        stagew = ctx.enter_context(tc.tile_pool(name="stagew", bufs=2))
         rows1 = ctx.enter_context(tc.tile_pool(name="rows1", bufs=4))
-        rows2 = ctx.enter_context(tc.tile_pool(name="rows2", bufs=3))
-        rows3 = ctx.enter_context(tc.tile_pool(name="rows3", bufs=4))
-        junkp = ctx.enter_context(tc.tile_pool(name="junkp", bufs=2))
+        rows2 = ctx.enter_context(tc.tile_pool(name="rows2", bufs=2))
+        rows3 = ctx.enter_context(tc.tile_pool(name="rows3", bufs=3))
+        junkp = ctx.enter_context(tc.tile_pool(name="junkp", bufs=1))
         plan = ctx.enter_context(tc.tile_pool(name="plan", bufs=2))
         small = ctx.enter_context(tc.tile_pool(name="small", bufs=8))
         ps_t = ctx.enter_context(tc.psum_pool(name="ps_t", bufs=5))
@@ -112,11 +54,13 @@ def tile_synapsemodel_pa_kernel(tc, z, attention_out, Wz, bz, gz, bz_ln, w1_deq,
         nc.vector.tensor_copy(out=identb[:], in_=ident[:])
         mhalf = const.tile([P, 1], F32, name="mhalf")
         nc.vector.memset(mhalf[:], -0.5)
-        vrows1 = const.tile([P, 512], BF16, name="vrows1")
+        eps = const.tile([P, 1], F32, name="eps")
+        nc.vector.memset(eps[:], LN_EPS)
+        vrows1 = const.tile([P, BANK], BF16, name="vrows1")
         nc.vector.memset(vrows1[:].bitcast(I32), 0)
         grows = const.tile([P, 256], BF16, name="grows")
         nc.vector.memset(grows[:].bitcast(I32), 0)
-        vrows2 = const.tile([P, 512], BF16, name="vrows2")
+        vrows2 = const.tile([P, BANK], BF16, name="vrows2")
         nc.vector.memset(vrows2[:].bitcast(I32), 0)
         nc.sync.dma_start(out=vrows1[0:2, :], in_=bz.rearrange("(a c) -> a c", a=2))
         nc.sync.dma_start(out=grows[0:4, :], in_=gz.rearrange("(a c) -> a c", a=4))
@@ -125,30 +69,44 @@ def tile_synapsemodel_pa_kernel(tc, z, attention_out, Wz, bz, gz, bz_ln, w1_deq,
         nc.scalar.dma_start(out=vrows2[4:6, :], in_=g1.rearrange("(a c) -> a c", a=2))
         nc.scalar.dma_start(out=vrows2[6:8, :], in_=b1_ln.rearrange("(a c) -> a c", a=2))
 
-        wz_v = Wz.rearrange("(a q e) k -> a e q k", q=P, e=2)
-
-        zq = keep.tile([P, 8 * 512], U32, name="zq", align_bytes=64)
-        zs = keep.tile([P, 8 * 512], U8, name="zs", align_bytes=64)
-        wq = keep.tile([P, 4 * 1024], U32, name="wq", align_bytes=64)
-        ws = keep.tile([P, 4 * 1024], U8, name="ws", align_bytes=64)
-        vq = keep.tile([P, 4 * 1024], U32, name="vq", align_bytes=64)
-        vs = keep.tile([P, 4 * 1024], U8, name="vs", align_bytes=64)
-        pq = keep.tile([P, 8 * 256], U32, name="pq", align_bytes=64)
-        pscl = keep.tile([P, 8 * 256], U8, name="pscl", align_bytes=64)
-        aq = keep.tile([P, 8 * 256], U32, name="aq", align_bytes=64)
-        ascl = keep.tile([P, 8 * 256], U8, name="ascl", align_bytes=64)
-        bc = const.tile([P, 4 * 1024], BF16, name="bc")
+        zq = keep.tile([P, TILES * 512], U32, name="zq", align_bytes=64)
+        zs = keep.tile([P, TILES * 512], U8, name="zs", align_bytes=64)
+        wq = keep.tile([P, PASSES * H], U32, name="wq", align_bytes=64)
+        ws = keep.tile([P, PASSES * H], U8, name="ws", align_bytes=64)
+        vq = keep.tile([P, PASSES * H], U32, name="vq", align_bytes=64)
+        vs = keep.tile([P, PASSES * H], U8, name="vs", align_bytes=64)
+        pq = keep.tile([P, TILES * 256], U32, name="pq", align_bytes=64)
+        pscl = keep.tile([P, TILES * 256], U8, name="pscl", align_bytes=64)
+        aq = keep.tile([P, TILES * 256], U32, name="aq", align_bytes=64)
+        ascl = keep.tile([P, TILES * 256], U8, name="ascl", align_bytes=64)
+        bc = const.tile([P, 4 * H], BF16, name="bc")
         gb = const.tile([P, 16], F32, name="gb")
+        wz_rows = Wz.rearrange("(a q e) k -> a e q k", q=P, e=2)
 
-        st = {}
+        live = {}
 
-        def bcast(r):
-            pb = ps_t.tile([P, 512], F32, tag="tp")
+        def load(kind, idx):
+            if kind == "a":
+                t = rawa.tile([P, H], BF16, tag="rawa")
+                src = attention_out[idx * P:(idx + 1) * P, :]
+            else:
+                t = raw.tile([P, D_IN], BF16, tag="raw")
+                if kind == "W":
+                    src = wz_rows[idx // 2, idx % 2]
+                elif kind == "z":
+                    src = z[idx * P:(idx + 1) * P, :]
+                else:
+                    src = w1_deq[idx * P:(idx + 1) * P, :]
+            nc.sync.dma_start(out=t[:], in_=src)
+            live[("raw", kind, idx)] = t
+
+        def spread_row(r):
+            pb = ps_t.tile([P, BANK], F32, tag="tp")
             nc.tensor.matmul(
                 pb[:], lhsT=identb[:, r:r + 1].to_broadcast([P, P]), rhs=(vrows1 if r < 2 else vrows2)[:],
                 start=True, stop=True,
             )
-            dst = bc[:, r * 512:(r + 1) * 512]
+            dst = bc[:, r * BANK:(r + 1) * BANK]
             if r < 2:
                 nc.vector.tensor_copy(
                     out=dst.rearrange("p (u e q) -> p u e q", u=2, e=2),
@@ -157,14 +115,12 @@ def tile_synapsemodel_pa_kernel(tc, z, attention_out, Wz, bz, gz, bz_ln, w1_deq,
             else:
                 nc.vector.tensor_copy(out=dst, in_=pb[:])
 
-        def op_CA():
-            bcast(0)
-            bcast(1)
+        def gain_columns():
             g32 = const.tile([P, 256], F32, name="g32")
             nc.vector.tensor_copy(
                 out=g32[:].rearrange("p (e q) -> p e q", e=2), in_=grows[:].rearrange("p (q e) -> p e q", e=2)
             )
-            pg = ps_t.tile([P, 512], F32, tag="tp")
+            pg = ps_t.tile([P, BANK], F32, tag="tp")
             for e in range(2):
                 nc.tensor.transpose(pg[:, e * P:(e + 1) * P], g32[:, e * P:(e + 1) * P], ident[:])
             nc.vector.tensor_copy(
@@ -172,63 +128,62 @@ def tile_synapsemodel_pa_kernel(tc, z, attention_out, Wz, bz, gz, bz_ln, w1_deq,
                 in_=pg[:, 0:256].rearrange("p (e r) -> p e r", e=2)[:, :, 0:8].rearrange("p e (w a) -> p w a e", w=2),
             )
 
-        def op_LD(kind, idx):
-            if kind == "a":
-                t = rawa.tile([P, H], BF16, tag="rawa")
-                src = attention_out[idx * P:(idx + 1) * P, :]
-            else:
-                t = raw.tile([P, D_IN], BF16, tag="raw")
-                if kind == "W":
-                    src = wz_v[idx // 2, idx % 2]
-                elif kind == "z":
-                    src = z[idx * P:(idx + 1) * P, :]
-                else:
-                    src = w1_deq[idx * P:(idx + 1) * P, :]
-            nc.sync.dma_start(out=t[:], in_=src)
-            st[("raw", kind, idx)] = t
-
-        def op_T(kind, idx, b):
-            words = st[("raw", kind, idx)][:].bitcast(F32)
-            xt = ps_t.tile([P, 512], F32, tag="tp")
+        def transpose_words(kind, idx, b):
+            if not 0 <= idx < TILES:
+                return
+            words = live[("raw", kind, idx)][:].bitcast(F32)
+            xt = ps_t.tile([P, BANK], F32, tag="tp")
             for s in range(4):
                 c0 = (4 * b + s) * P
                 nc.tensor.transpose(xt[:, s * P:(s + 1) * P], words[:, c0:c0 + P], ident[:])
-            st[("xt", kind, idx, b)] = xt
-
-        def op_EX(kind, idx, b, eng):
-            if ("grp", kind, idx) not in st:
-                if kind == "a":
-                    grouped = stagea.tile([P, H], BF16, tag="grpa", align_bytes=64)
+            src = xt[:].rearrange("p (g u r) -> p g r u", g=2, u=2)
+            if kind in ("W", "w"):
+                key = ("grp", kind, idx // 4)
+                if key not in live:
+                    grouped_w = stagew.tile([P, 4 * D_IN], BF16, tag="grpw", align_bytes=64)
+                    live[key] = grouped_w
+                dst = live[key][:].bitcast(F32).rearrange("p (g j r u) -> p g j r u", g=4, j=4, u=2)[
+                    :, 2 * b:2 * b + 2, idx % 4
+                ]
+                if b == 1:
+                    nc.vector.tensor_copy(out=dst, in_=src)
                 else:
-                    grouped = stage.tile([P, D_IN], BF16, tag="grp", align_bytes=64)
-                st[("grp", kind, idx)] = grouped
-            gw = st[("grp", kind, idx)][:].bitcast(F32)
-            dst = gw[:, b * 512:(b + 1) * 512].rearrange("p (g r u) -> p g r u", g=2, u=2)
-            src = st[("xt", kind, idx, b)][:].rearrange("p (g u r) -> p g r u", g=2, u=2)
-            if eng == "V":
-                nc.vector.tensor_copy(out=dst, in_=src)
+                    nc.scalar.copy(out=dst, in_=src)
             else:
+                key = ("grp", kind, idx)
+                if key not in live:
+                    if kind == "a":
+                        grouped = stage.tile([P, H], BF16, tag="grpa", align_bytes=64)
+                    else:
+                        grouped = stage.tile([P, D_IN], BF16, tag="grp", align_bytes=64)
+                    live[key] = grouped
+                dst = live[key][:].bitcast(F32)[:, b * BANK:(b + 1) * BANK].rearrange(
+                    "p (g r u) -> p g r u", g=2, u=2
+                )
                 nc.scalar.copy(out=dst, in_=src)
 
-        def op_Q(kind, idx):
-            grouped = st[("grp", kind, idx)]
-            if kind == "z":
-                sl = slice(idx * 512, (idx + 1) * 512)
-                nc.vector.quantize_mx(out=zq[:, sl].bitcast(FP8X4), scales=zs[:, sl], in_=grouped[:])
-            elif kind == "a":
-                sl = slice(idx * 256, (idx + 1) * 256)
-                nc.vector.quantize_mx(out=aq[:, sl].bitcast(FP8X4), scales=ascl[:, sl], in_=grouped[:])
-            else:
-                cq, cs = (wq, ws) if kind == "W" else (vq, vs)
-                for g in range(4):
-                    sl = slice(g * 1024 + idx * P, g * 1024 + (idx + 1) * P)
-                    nc.vector.quantize_mx(
-                        out=cq[:, sl].bitcast(FP8X4), scales=cs[:, sl], in_=grouped[:, g * 512:(g + 1) * 512]
-                    )
+        def quantise_weights(kind, half):
+            cq, cs = (wq, ws) if kind == "W" else (vq, vs)
+            for g in range(PASSES):
+                sl = slice(g * H + half * BANK, g * H + (half + 1) * BANK)
+                nc.vector.quantize_mx(
+                    out=cq[:, sl].bitcast(FP8X4), scales=cs[:, sl],
+                    in_=live[("grp", kind, half)][:, g * D_IN:(g + 1) * D_IN],
+                )
 
-        def op_M(stg, i, n):
-            acc = ps_a.tile([P, 512], F32, tag="acc")
-            for g in range(4):
+        def quantise_rows(kind, idx):
+            if not 0 <= idx < TILES:
+                return
+            words = 512 if kind == "z" else 256
+            cq, cs = (zq, zs) if kind == "z" else (aq, ascl)
+            sl = slice(idx * words, (idx + 1) * words)
+            nc.vector.quantize_mx(out=cq[:, sl].bitcast(FP8X4), scales=cs[:, sl], in_=live[("grp", kind, idx)][:])
+
+        def mx_group(stg, i, n):
+            if not 0 <= i < TILES:
+                return
+            acc = ps_a.tile([P, BANK], F32, tag="acc")
+            for g in range(PASSES):
                 if stg == 1:
                     c0 = i * 512 + g * P
                     lq, ls, rq, rs = zq, zs, wq, ws
@@ -237,170 +192,157 @@ def tile_synapsemodel_pa_kernel(tc, z, attention_out, Wz, bz, gz, bz_ln, w1_deq,
                     lq, ls = (pq, pscl) if g < 2 else (aq, ascl)
                     rq, rs = vq, vs
                 sl = slice(c0, c0 + P)
-                sr = slice(g * 1024 + n * 512, g * 1024 + (n + 1) * 512)
+                sr = slice(g * H + n * BANK, g * H + (n + 1) * BANK)
                 nc.tensor.matmul_mx(
                     out=acc[:], lhsT=lq[:, sl].bitcast(FP8X4), lhsT_scale=ls[:, sl],
-                    rhs=rq[:, sr].bitcast(FP8X4), rhs_scale=rs[:, sr], start=(g == 0), stop=(g == 3),
+                    rhs=rq[:, sr].bitcast(FP8X4), rhs_scale=rs[:, sr], start=(g == 0), stop=(g == PASSES - 1),
                 )
-            st[("acc", stg, i, n)] = acc
-
-        def op_A(stg, i, n):
-            if ("y", stg, i) not in st:
+            if n == 0:
                 if stg == 1:
                     y = rows1.tile([P, H], F32, tag="y1")
                 else:
                     y = rows2.tile([P, H], F32, tag="y2")
-                s = small.tile([P, 2], F32, tag="s")
-                st[("y", stg, i)] = y
-                st[("s", stg, i)] = s
-            off = (stg - 1) * 1024 + n * 512
+                sums = small.tile([P, 2], F32, tag="sums")
+                live[("y", stg, i)] = y
+                live[("sums", stg, i)] = sums
+            off = (stg - 1) * H + n * BANK
             nc.vector.scalar_tensor_tensor(
-                out=st[("y", stg, i)][:, n * 512:(n + 1) * 512], in0=st[("acc", stg, i, n)][:], scalar=1.0,
-                in1=bc[:, off:off + 512], op0=ALU.mult, op1=ALU.add, accum_out=st[("s", stg, i)][:, n:n + 1],
+                out=live[("y", stg, i)][:, n * BANK:(n + 1) * BANK], in0=acc[:], scalar=1.0,
+                in1=bc[:, off:off + BANK], op0=ALU.mult, op1=ALU.add, accum_out=live[("sums", stg, i)][:, n:n + 1],
             )
 
-        def op_NM(stg, i):
-            s = st[("s", stg, i)]
-            nm = small.tile([P, 1], F32, tag="nm")
-            nc.vector.tensor_scalar(
-                out=nm[:], in0=s[:, 0:1], scalar1=s[:, 1:2], scalar2=-1.0 / H, op0=ALU.add, op1=ALU.mult
+        def stats(stg, i):
+            if not 0 <= i < TILES:
+                return
+            junk2 = small.tile([P, 2], F32, tag="junk2")
+            nmean = small.tile([P, 1], F32, tag="nmean")
+            nc.scalar.activation(
+                out=junk2[:], in_=live[("sums", stg, i)][:], func=ACT.Identity, scale=-1.0 / H, accum_out=nmean[:]
             )
-            st[("nm", stg, i)] = nm
-
-        def op_B(stg, i):
             junk = junkp.tile([P, H], BF16, tag="junk")
             ssq = small.tile([P, 1], F32, tag="ssq")
             nc.scalar.activation(
-                out=junk[:], in_=st[("y", stg, i)][:], func=ACT.Square, bias=st[("nm", stg, i)][:], scale=1.0,
-                accum_out=ssq[:],
+                out=junk[:], in_=live[("y", stg, i)][:], func=ACT.Square, bias=nmean[:], scale=1.0, accum_out=ssq[:]
             )
-            st[("ssq", stg, i)] = ssq
+            veps = small.tile([P, 1], F32, tag="veps")
+            nc.scalar.activation(out=veps[:], in_=ssq[:], func=ACT.Identity, scale=1.0 / H, bias=eps[:])
+            live[("nmean", stg, i)] = nmean
+            live[("veps", stg, i)] = veps
 
-        def op_R(stg, i):
-            ve = small.tile([P, 1], F32, tag="ve")
-            nc.gpsimd.tensor_scalar(
-                out=ve[:], in0=st[("ssq", stg, i)][:], scalar1=1.0 / H, scalar2=LN_EPS, op0=ALU.mult, op1=ALU.add
-            )
+        def rstd_of(stg, i):
+            if not 0 <= i < TILES:
+                return
             rstd = small.tile([P, 1], F32, tag="rstd")
-            nc.gpsimd.tensor_tensor(out=rstd[:], in0=ve[:], in1=mhalf[:], op=ALU.pow)
-            st[("rstd", stg, i)] = rstd
+            nc.gpsimd.tensor_tensor(out=rstd[:], in0=live[("veps", stg, i)][:], in1=mhalf[:], op=ALU.pow)
+            live[("rstd", stg, i)] = rstd
+            if stg == 1:
+                y = live[("y", 1, i)]
+                nc.gpsimd.tensor_scalar(
+                    out=y[:], in0=y[:], scalar1=live[("nmean", 1, i)][:], scalar2=rstd[:], op0=ALU.add, op1=ALU.mult
+                )
 
-        def op_C1(i, eng):
-            y = st[("y", 1, i)]
-            e = nc.vector if eng == "V" else nc.gpsimd
-            e.tensor_scalar(
-                out=y[:], in0=y[:], scalar1=st[("nm", 1, i)][:], scalar2=st[("rstd", 1, i)][:],
-                op0=ALU.add, op1=ALU.mult,
-            )
-
-        def op_TP(i, g):
-            tp = ps_t.tile([P, 512], F32, tag="tp")
+        def transpose_rows(i, g):
+            if not 0 <= i < TILES:
+                return
+            tp = ps_t.tile([P, BANK], F32, tag="tp")
             for t in range(4):
                 j = 4 * g + t
-                nc.tensor.transpose(tp[:, t * P:(t + 1) * P], st[("y", 1, i)][:, j * P:(j + 1) * P], ident[:])
-            st[("tp", i, g)] = tp
-
-        def op_E1(i, g, eng):
-            if ("planar", i) not in st:
+                nc.tensor.transpose(tp[:, t * P:(t + 1) * P], live[("y", 1, i)][:, j * P:(j + 1) * P], ident[:])
+            if g == 0:
                 planar = plan.tile([P, H], BF16, tag="planar")
-                st[("planar", i)] = planar
+                live[("planar", i)] = planar
             for t in range(4):
                 j = 4 * g + t
-                dst = st[("planar", i)][:, j * P:(j + 1) * P]
-                src = st[("tp", i, g)][:, t * P:(t + 1) * P]
-                if eng == "V":
-                    nc.vector.tensor_scalar(
-                        out=dst, in0=src, scalar1=gb[:, j:j + 1], scalar2=gb[:, 8 + j:9 + j], op0=ALU.mult, op1=ALU.add
-                    )
-                else:
-                    nc.scalar.activation(
-                        out=dst, in_=src, func=ACT.Identity, scale=gb[:, j:j + 1], bias=gb[:, 8 + j:9 + j]
-                    )
+                nc.scalar.activation(
+                    out=live[("planar", i)][:, j * P:(j + 1) * P], in_=tp[:, t * P:(t + 1) * P], func=ACT.Identity,
+                    scale=gb[:, j:j + 1], bias=gb[:, 8 + j:9 + j],
+                )
 
-        def op_RG(i, eng):
+        def regroup(i):
+            if not 0 <= i < TILES:
+                return
             gp = plan.tile([P, H], BF16, tag="gp", align_bytes=64)
             nc.vector.tensor_copy(
                 out=gp[:].rearrange("p (g c t) -> p g c t", g=2, t=4),
-                in_=st[("planar", i)][:].rearrange("p (g t c) -> p g c t", g=2, t=4),
+                in_=live[("planar", i)][:].rearrange("p (g t c) -> p g c t", g=2, t=4),
             )
-            st[("gp", i)] = gp
-
-        def op_QP(i):
             sl = slice(i * 256, (i + 1) * 256)
-            nc.vector.quantize_mx(out=pq[:, sl].bitcast(FP8X4), scales=pscl[:, sl], in_=st[("gp", i)][:])
+            nc.vector.quantize_mx(out=pq[:, sl].bitcast(FP8X4), scales=pscl[:, sl], in_=gp[:])
 
-        def op_C2(i):
+        def gain(i):
+            if not 0 <= i < TILES:
+                return
             t2 = rows3.tile([P, H], F32, tag="t2")
             nc.vector.scalar_tensor_tensor(
-                out=t2[:], in0=st[("y", 2, i)][:], scalar=st[("nm", 2, i)][:], in1=bc[:, 2048:3072],
+                out=t2[:], in0=live[("y", 2, i)][:], scalar=live[("nmean", 2, i)][:], in1=bc[:, 2 * H:3 * H],
                 op0=ALU.add, op1=ALU.mult,
             )
-            st[("t2", i)] = t2
+            live[("t2", i)] = t2
 
-        def op_D2(i):
-            t2 = st[("t2", i)]
+        def shift(i):
+            if not 0 <= i < TILES:
+                return
+            t2 = live[("t2", i)]
             nc.vector.scalar_tensor_tensor(
-                out=t2[:], in0=t2[:], scalar=st[("rstd", 2, i)][:], in1=bc[:, 3072:4096], op0=ALU.mult, op1=ALU.add
+                out=t2[:], in0=t2[:], scalar=live[("rstd", 2, i)][:], in1=bc[:, 3 * H:4 * H], op0=ALU.mult, op1=ALU.add
             )
 
-        def op_E2(i):
-            t2 = st[("t2", i)]
+        def gelu_store(i):
+            if not 0 <= i < TILES:
+                return
+            t2 = live[("t2", i)]
             nc.scalar.activation(out=t2[:], in_=t2[:], func=ACT.Gelu)
+            nc.sync.dma_start(out=out[i * P:(i + 1) * P, :], in_=t2[:])
 
-        def op_ST(i):
-            nc.sync.dma_start(out=out[i * P:(i + 1) * P, :], in_=st[("t2", i)][:])
+        for j in range(TILES):
+            load("W", j)
+        for r in range(-AHEAD_Z, TILES - AHEAD_A):
+            if r + AHEAD_Z < TILES:
+                load("z", r + AHEAD_Z)
+            for j in (2 * (r + AHEAD_Z), 2 * (r + AHEAD_Z) + 1):
+                if j < TILES:
+                    load("w", j)
+                if j % 2 == 0 and r + AHEAD_A >= 0:
+                    load("a", r + AHEAD_A)
 
-        for step in SCHEDULE:
-            k = step[0]
-            a = step[1:]
-            if k == "LD":
-                op_LD(*a)
-            elif k == "CA":
-                op_CA()
-            elif k == "CB":
-                bcast(*a)
-            elif k == "T":
-                op_T(*a)
-            elif k == "EX":
-                op_EX(*a)
-            elif k == "Q":
-                op_Q(*a)
-            elif k == "M1":
-                op_M(1, *a)
-            elif k == "M2":
-                op_M(2, *a)
-            elif k == "A1":
-                op_A(1, *a)
-            elif k == "A2":
-                op_A(2, *a)
-            elif k == "NM1":
-                op_NM(1, *a)
-            elif k == "NM2":
-                op_NM(2, *a)
-            elif k == "B1":
-                op_B(1, *a)
-            elif k == "B2":
-                op_B(2, *a)
-            elif k == "R1":
-                op_R(1, *a)
-            elif k == "R2":
-                op_R(2, *a)
-            elif k == "C1":
-                op_C1(*a)
-            elif k == "TP":
-                op_TP(*a)
-            elif k == "E1":
-                op_E1(*a)
-            elif k == "RG":
-                op_RG(*a)
-            elif k == "QP":
-                op_QP(*a)
-            elif k == "C2":
-                op_C2(*a)
-            elif k == "D2":
-                op_D2(*a)
-            elif k == "E2":
-                op_E2(*a)
-            else:
-                assert k == "ST"
-                op_ST(*a)
+        for j in range(TILES):
+            transpose_words("W", j, 0)
+            transpose_words("W", j, 1)
+            if j == 1:
+                spread_row(0)
+                spread_row(1)
+                gain_columns()
+            if j >= 2:
+                spread_row(j)
+            if j == 4:
+                quantise_weights("W", 0)
+
+        for r in range(-AHEAD_Z, TILES + DRAIN_ROUNDS):
+            w_first = 2 * (r + AHEAD_Z)
+            mx_group(2, r, 0)
+            regroup(r + 1)
+            transpose_words("z", r + AHEAD_Z, 0)
+            rstd_of(2, r - 1)
+            transpose_words("z", r + AHEAD_Z, 1)
+            if w_first == 0:
+                quantise_weights("W", 1)
+            elif w_first in (4, 8):
+                quantise_weights("w", w_first // 4 - 1)
+            transpose_words("w", w_first, 0)
+            transpose_words("w", w_first, 1)
+            mx_group(2, r, 1)
+            stats(1, r + AHEAD_M1 - 1)
+            rstd_of(1, r + AHEAD_M1 - 1)
+            gelu_store(r - 2)
+            transpose_words("a", r + AHEAD_A, 0)
+            mx_group(1, r + AHEAD_M1, 0)
+            transpose_rows(r + AHEAD_ROWS, 0)
+            transpose_words("w", w_first + 1, 0)
+            transpose_words("w", w_first + 1, 1)
+            quantise_rows("z", r + AHEAD_Z)
+            stats(2, r)
+            mx_group(1, r + AHEAD_M1, 1)
+            quantise_rows("a", r + AHEAD_A)
+            shift(r - 1)
+            gain(r)
+            transpose_rows(r + AHEAD_ROWS, 1)

@@ -299,11 +299,11 @@ def tile_synapsemodel_pa_kernel(tc, z, attention_out, Wz, bz, gz, bz_ln, w1_deq,
         for r in range(-AHEAD_Z, TILES - AHEAD_A):
             if r + AHEAD_Z < TILES:
                 load("z", r + AHEAD_Z)
+            if r + AHEAD_A >= 0:
+                load("a", r + AHEAD_A)
             for j in (2 * (r + AHEAD_Z), 2 * (r + AHEAD_Z) + 1):
                 if j < TILES:
                     load("w", j)
-                if j % 2 == 0 and r + AHEAD_A >= 0:
-                    load("a", r + AHEAD_A)
 
         for j in range(TILES):
             transpose_words("W", j, 0)
@@ -319,30 +319,30 @@ def tile_synapsemodel_pa_kernel(tc, z, attention_out, Wz, bz, gz, bz_ln, w1_deq,
 
         for r in range(-AHEAD_Z, TILES + DRAIN_ROUNDS):
             w_first = 2 * (r + AHEAD_Z)
+            gelu_store(r - 2)
             mx_group(2, r, 0)
             regroup(r + 1)
-            transpose_words("z", r + AHEAD_Z, 0)
+            mx_group(2, r, 1)
+            gain(r - 1)
             rstd_of(2, r - 1)
+            transpose_words("z", r + AHEAD_Z, 0)
             transpose_words("z", r + AHEAD_Z, 1)
             if w_first == 0:
                 quantise_weights("W", 1)
             elif w_first in (4, 8):
                 quantise_weights("w", w_first // 4 - 1)
+            rstd_of(1, r + AHEAD_M1 - 1)
+            transpose_words("a", r + AHEAD_A, 0)
             transpose_words("w", w_first, 0)
             transpose_words("w", w_first, 1)
-            mx_group(2, r, 1)
-            stats(1, r + AHEAD_M1 - 1)
-            rstd_of(1, r + AHEAD_M1 - 1)
-            gelu_store(r - 2)
-            transpose_words("a", r + AHEAD_A, 0)
+            stats(2, r)
             mx_group(1, r + AHEAD_M1, 0)
+            quantise_rows("z", r + AHEAD_Z)
+            mx_group(1, r + AHEAD_M1, 1)
             transpose_rows(r + AHEAD_ROWS, 0)
+            shift(r - 1)
+            transpose_rows(r + AHEAD_ROWS, 1)
             transpose_words("w", w_first + 1, 0)
             transpose_words("w", w_first + 1, 1)
-            quantise_rows("z", r + AHEAD_Z)
-            stats(2, r)
-            mx_group(1, r + AHEAD_M1, 1)
             quantise_rows("a", r + AHEAD_A)
-            shift(r - 1)
-            gain(r)
-            transpose_rows(r + AHEAD_ROWS, 1)
+            stats(1, r + AHEAD_M1)

@@ -19,6 +19,8 @@ H = 1024
 BANK = 512
 PASSES = D_IN // 512
 TILES = N_TOK // P
+Z_WORDS = PASSES * P
+HALF_WORDS = Z_WORDS // 2
 LN_EPS = 1e-5
 FLOPS = 2 * N_TOK * D_IN * H + 2 * N_TOK * D_IN * H
 
@@ -69,16 +71,16 @@ def tile_synapsemodel_pa_kernel(tc, z, attention_out, Wz, bz, gz, bz_ln, w1_deq,
         nc.scalar.dma_start(out=vrows2[4:6, :], in_=g1.rearrange("(a c) -> a c", a=2))
         nc.scalar.dma_start(out=vrows2[6:8, :], in_=b1_ln.rearrange("(a c) -> a c", a=2))
 
-        zq = keep.tile([P, TILES * 512], U32, name="zq", align_bytes=64)
-        zs = keep.tile([P, TILES * 512], U8, name="zs", align_bytes=64)
+        zq = keep.tile([P, TILES * Z_WORDS], U32, name="zq", align_bytes=64)
+        zs = keep.tile([P, TILES * Z_WORDS], U8, name="zs", align_bytes=64)
         wq = keep.tile([P, PASSES * H], U32, name="wq", align_bytes=64)
         ws = keep.tile([P, PASSES * H], U8, name="ws", align_bytes=64)
         vq = keep.tile([P, PASSES * H], U32, name="vq", align_bytes=64)
         vs = keep.tile([P, PASSES * H], U8, name="vs", align_bytes=64)
-        pq = keep.tile([P, TILES * 256], U32, name="pq", align_bytes=64)
-        pscl = keep.tile([P, TILES * 256], U8, name="pscl", align_bytes=64)
-        aq = keep.tile([P, TILES * 256], U32, name="aq", align_bytes=64)
-        ascl = keep.tile([P, TILES * 256], U8, name="ascl", align_bytes=64)
+        pq = keep.tile([P, TILES * HALF_WORDS], U32, name="pq", align_bytes=64)
+        pscl = keep.tile([P, TILES * HALF_WORDS], U8, name="pscl", align_bytes=64)
+        aq = keep.tile([P, TILES * HALF_WORDS], U32, name="aq", align_bytes=64)
+        ascl = keep.tile([P, TILES * HALF_WORDS], U8, name="ascl", align_bytes=64)
         bc = const.tile([P, 4 * H], BF16, name="bc")
         gb = const.tile([P, 16], F32, name="gb")
         wz_rows = Wz.rearrange("(a q e) k -> a e q k", q=P, e=2)
@@ -100,14 +102,14 @@ def tile_synapsemodel_pa_kernel(tc, z, attention_out, Wz, bz, gz, bz_ln, w1_deq,
             nc.sync.dma_start(out=t[:], in_=src)
             live[("raw", kind, idx)] = t
 
-        def spread_row(r):
+        def spread_row(row):
             pb = ps_t.tile([P, BANK], F32, tag="tp")
             nc.tensor.matmul(
-                pb[:], lhsT=identb[:, r:r + 1].to_broadcast([P, P]), rhs=(vrows1 if r < 2 else vrows2)[:],
+                pb[:], lhsT=identb[:, row:row + 1].to_broadcast([P, P]), rhs=(vrows1 if row < 2 else vrows2)[:],
                 start=True, stop=True,
             )
-            dst = bc[:, r * BANK:(r + 1) * BANK]
-            if r < 2:
+            dst = bc[:, row * BANK:(row + 1) * BANK]
+            if row < 2:
                 nc.vector.tensor_copy(
                     out=dst.rearrange("p (u e q) -> p u e q", u=2, e=2),
                     in_=pb[:].rearrange("p (u q e) -> p u e q", u=2, e=2),
@@ -162,33 +164,36 @@ def tile_synapsemodel_pa_kernel(tc, z, attention_out, Wz, bz, gz, bz_ln, w1_deq,
                 )
                 nc.scalar.copy(out=dst, in_=src)
 
-        def quantise_weights(kind, half):
+        def quantise_weights(kind, n):
             cq, cs = (wq, ws) if kind == "W" else (vq, vs)
             for g in range(PASSES):
-                sl = slice(g * H + half * BANK, g * H + (half + 1) * BANK)
+                sl = slice(g * H + n * BANK, g * H + (n + 1) * BANK)
                 nc.vector.quantize_mx(
                     out=cq[:, sl].bitcast(FP8X4), scales=cs[:, sl],
-                    in_=live[("grp", kind, half)][:, g * D_IN:(g + 1) * D_IN],
+                    in_=live[("grp", kind, n)][:, g * D_IN:(g + 1) * D_IN],
                 )
 
         def quantise_rows(kind, idx):
             if not 0 <= idx < TILES:
                 return
-            words = 512 if kind == "z" else 256
+            words = Z_WORDS if kind == "z" else HALF_WORDS
             cq, cs = (zq, zs) if kind == "z" else (aq, ascl)
             sl = slice(idx * words, (idx + 1) * words)
             nc.vector.quantize_mx(out=cq[:, sl].bitcast(FP8X4), scales=cs[:, sl], in_=live[("grp", kind, idx)][:])
 
-        def mx_group(stg, i, n):
+        def mx_passes(stg, i, n, first, end):
             if not 0 <= i < TILES:
                 return
-            acc = ps_a.tile([P, BANK], F32, tag="acc")
-            for g in range(PASSES):
+            if first == 0:
+                acc = ps_a.tile([P, BANK], F32, tag="acc")
+                live[("acc", stg, i, n)] = acc
+            acc = live[("acc", stg, i, n)]
+            for g in range(first, end):
                 if stg == 1:
-                    c0 = i * 512 + g * P
+                    c0 = i * Z_WORDS + g * P
                     lq, ls, rq, rs = zq, zs, wq, ws
                 else:
-                    c0 = i * 256 + (g % 2) * P
+                    c0 = i * HALF_WORDS + (g % 2) * P
                     lq, ls = (pq, pscl) if g < 2 else (aq, ascl)
                     rq, rs = vq, vs
                 sl = slice(c0, c0 + P)
@@ -197,6 +202,8 @@ def tile_synapsemodel_pa_kernel(tc, z, attention_out, Wz, bz, gz, bz_ln, w1_deq,
                     out=acc[:], lhsT=lq[:, sl].bitcast(FP8X4), lhsT_scale=ls[:, sl],
                     rhs=rq[:, sr].bitcast(FP8X4), rhs_scale=rs[:, sr], start=(g == 0), stop=(g == PASSES - 1),
                 )
+            if end < PASSES:
+                return
             if n == 0:
                 if stg == 1:
                     y = rows1.tile([P, H], F32, tag="y1")
@@ -245,17 +252,17 @@ def tile_synapsemodel_pa_kernel(tc, z, attention_out, Wz, bz, gz, bz_ln, w1_deq,
             if not 0 <= i < TILES:
                 return
             tp = ps_t.tile([P, BANK], F32, tag="tp")
-            for t in range(4):
-                j = 4 * g + t
-                nc.tensor.transpose(tp[:, t * P:(t + 1) * P], live[("y", 1, i)][:, j * P:(j + 1) * P], ident[:])
+            for v in range(4):
+                blk = 4 * g + v
+                nc.tensor.transpose(tp[:, v * P:(v + 1) * P], live[("y", 1, i)][:, blk * P:(blk + 1) * P], ident[:])
             if g == 0:
                 planar = plan.tile([P, H], BF16, tag="planar")
                 live[("planar", i)] = planar
-            for t in range(4):
-                j = 4 * g + t
+            for v in range(4):
+                blk = 4 * g + v
                 nc.scalar.activation(
-                    out=live[("planar", i)][:, j * P:(j + 1) * P], in_=tp[:, t * P:(t + 1) * P], func=ACT.Identity,
-                    scale=gb[:, j:j + 1], bias=gb[:, 8 + j:9 + j],
+                    out=live[("planar", i)][:, blk * P:(blk + 1) * P], in_=tp[:, v * P:(v + 1) * P],
+                    func=ACT.Identity, scale=gb[:, blk:blk + 1], bias=gb[:, 8 + blk:9 + blk],
                 )
 
         def regroup(i):
@@ -266,7 +273,7 @@ def tile_synapsemodel_pa_kernel(tc, z, attention_out, Wz, bz, gz, bz_ln, w1_deq,
                 out=gp[:].rearrange("p (g c t) -> p g c t", g=2, t=4),
                 in_=live[("planar", i)][:].rearrange("p (g t c) -> p g c t", g=2, t=4),
             )
-            sl = slice(i * 256, (i + 1) * 256)
+            sl = slice(i * HALF_WORDS, (i + 1) * HALF_WORDS)
             nc.vector.quantize_mx(out=pq[:, sl].bitcast(FP8X4), scales=pscl[:, sl], in_=gp[:])
 
         def gain(i):
@@ -319,30 +326,36 @@ def tile_synapsemodel_pa_kernel(tc, z, attention_out, Wz, bz, gz, bz_ln, w1_deq,
 
         for r in range(-AHEAD_Z, TILES + DRAIN_ROUNDS):
             w_first = 2 * (r + AHEAD_Z)
-            gelu_store(r - 2)
-            mx_group(2, r, 0)
+            m = r + AHEAD_M1
+            mx_passes(2, r, 0, 0, PASSES)
             regroup(r + 1)
-            mx_group(2, r, 1)
-            gain(r - 1)
-            rstd_of(2, r - 1)
             transpose_words("z", r + AHEAD_Z, 0)
+            rstd_of(2, r - 1)
             transpose_words("z", r + AHEAD_Z, 1)
             if w_first == 0:
                 quantise_weights("W", 1)
             elif w_first in (4, 8):
                 quantise_weights("w", w_first // 4 - 1)
-            rstd_of(1, r + AHEAD_M1 - 1)
+            mx_passes(2, r, 1, 0, PASSES)
+            stats(1, m - 1)
+            rstd_of(1, m - 1)
+            gelu_store(r - 2)
+            mx_passes(1, m, 0, 0, 1)
             transpose_words("a", r + AHEAD_A, 0)
+            mx_passes(1, m, 0, 1, 2)
             transpose_words("w", w_first, 0)
+            mx_passes(1, m, 0, 2, 3)
             transpose_words("w", w_first, 1)
-            stats(2, r)
-            mx_group(1, r + AHEAD_M1, 0)
-            quantise_rows("z", r + AHEAD_Z)
-            mx_group(1, r + AHEAD_M1, 1)
+            mx_passes(1, m, 0, 3, PASSES)
             transpose_rows(r + AHEAD_ROWS, 0)
-            shift(r - 1)
-            transpose_rows(r + AHEAD_ROWS, 1)
+            quantise_rows("z", r + AHEAD_Z)
+            stats(2, r)
+            mx_passes(1, m, 1, 0, 1)
             transpose_words("w", w_first + 1, 0)
+            mx_passes(1, m, 1, 1, 2)
             transpose_words("w", w_first + 1, 1)
+            mx_passes(1, m, 1, 2, PASSES)
             quantise_rows("a", r + AHEAD_A)
-            stats(1, r + AHEAD_M1)
+            shift(r - 1)
+            gain(r)
+            transpose_rows(r + AHEAD_ROWS, 1)

from contextlib import ExitStack

import concourse.mybir as mybir
from concourse.masks import make_identity

F32 = mybir.dt.float32
BF16 = mybir.dt.bfloat16
U32 = mybir.dt.uint32
U8 = mybir.dt.uint8
I32 = mybir.dt.int32
FP8X4 = mybir.dt.float8_e4m3fn_x4
ALU = mybir.AluOpType
ACT = mybir.ActivationFunctionType

P = 128
N_TOK = 1024
D_IN = 2048
H = 1024
BANK = 512
PASSES = D_IN // 512
TILES = N_TOK // P
Z_WORDS = PASSES * P
HALF_WORDS = Z_WORDS // 2
LN_EPS = 1e-5
FLOPS = 2 * N_TOK * D_IN * H + 2 * N_TOK * D_IN * H

AHEAD_Z = 5
AHEAD_M1 = 4
AHEAD_A = 3
AHEAD_ROWS = 2
DRAIN_ROUNDS = 2


def tile_synapsemodel_pa_kernel(tc, z, attention_out, Wz, bz, gz, bz_ln, w1_deq, b1, g1, b1_ln, out):
    nc = tc.nc
    with ExitStack() as ctx:
        const = ctx.enter_context(tc.tile_pool(name="const", bufs=1))
        keep = ctx.enter_context(tc.tile_pool(name="keep", bufs=1))
        raw = ctx.enter_context(tc.tile_pool(name="raw", bufs=6))
        rawa = ctx.enter_context(tc.tile_pool(name="rawa", bufs=4))
        stage = ctx.enter_context(tc.tile_pool(name="stage", bufs=3))
        stagew = ctx.enter_context(tc.tile_pool(name="stagew", bufs=2))
        rows1 = ctx.enter_context(tc.tile_pool(name="rows1", bufs=4))
        rows2 = ctx.enter_context(tc.tile_pool(name="rows2", bufs=2))
        rows3 = ctx.enter_context(tc.tile_pool(name="rows3", bufs=3))
        junkp = ctx.enter_context(tc.tile_pool(name="junkp", bufs=1))
        plan = ctx.enter_context(tc.tile_pool(name="plan", bufs=2))
        small = ctx.enter_context(tc.tile_pool(name="small", bufs=8))
        ps_t = ctx.enter_context(tc.psum_pool(name="ps_t", bufs=5))
        ps_a = ctx.enter_context(tc.psum_pool(name="ps_a", bufs=3))
        ctx.enter_context(tc.manual_schedule())

        ident = const.tile([P, P], F32, name="ident")
        make_identity(nc, ident[:])
        identb = const.tile([P, P], BF16, name="identb")
        nc.vector.tensor_copy(out=identb[:], in_=ident[:])
        mhalf = const.tile([P, 1], F32, name="mhalf")
        nc.vector.memset(mhalf[:], -0.5)
        eps = const.tile([P, 1], F32, name="eps")
        nc.vector.memset(eps[:], LN_EPS)
        vrows1 = const.tile([P, BANK], BF16, name="vrows1")
        nc.vector.memset(vrows1[:].bitcast(I32), 0)
        grows = const.tile([P, 256], BF16, name="grows")
        nc.vector.memset(grows[:].bitcast(I32), 0)
        vrows2 = const.tile([P, BANK], BF16, name="vrows2")
        nc.vector.memset(vrows2[:].bitcast(I32), 0)
        nc.sync.dma_start(out=vrows1[0:2, :], in_=bz.rearrange("(a c) -> a c", a=2))
        nc.sync.dma_start(out=grows[0:4, :], in_=gz.rearrange("(a c) -> a c", a=4))
        nc.sync.dma_start(out=grows[4:8, :], in_=bz_ln.rearrange("(a c) -> a c", a=4))
        nc.scalar.dma_start(out=vrows2[2:4, :], in_=b1.rearrange("(a c) -> a c", a=2))
        nc.scalar.dma_start(out=vrows2[4:6, :], in_=g1.rearrange("(a c) -> a c", a=2))
        nc.scalar.dma_start(out=vrows2[6:8, :], in_=b1_ln.rearrange("(a c) -> a c", a=2))

        zq = keep.tile([P, TILES * Z_WORDS], U32, name="zq", align_bytes=64)
        zs = keep.tile([P, TILES * Z_WORDS], U8, name="zs", align_bytes=64)
        wq = keep.tile([P, PASSES * H], U32, name="wq", align_bytes=64)
        ws = keep.tile([P, PASSES * H], U8, name="ws", align_bytes=64)
        vq = keep.tile([P, PASSES * H], U32, name="vq", align_bytes=64)
        vs = keep.tile([P, PASSES * H], U8, name="vs", align_bytes=64)
        pq = keep.tile([P, TILES * HALF_WORDS], U32, name="pq", align_bytes=64)
        pscl = keep.tile([P, TILES * HALF_WORDS], U8, name="pscl", align_bytes=64)
        aq = keep.tile([P, TILES * HALF_WORDS], U32, name="aq", align_bytes=64)
        ascl = keep.tile([P, TILES * HALF_WORDS], U8, name="ascl", align_bytes=64)
        bc = const.tile([P, 4 * H], BF16, name="bc")
        gb = const.tile([P, 16], F32, name="gb")
        wz_rows = Wz.rearrange("(a q e) k -> a e q k", q=P, e=2)

        live = {}

        def load(kind, idx):
            if kind == "a":
                t = rawa.tile([P, H], BF16, tag="rawa")
                src = attention_out[idx * P:(idx + 1) * P, :]
            else:
                t = raw.tile([P, D_IN], BF16, tag="raw")
                if kind == "W":
                    src = wz_rows[idx // 2, idx % 2]
                elif kind == "z":
                    src = z[idx * P:(idx + 1) * P, :]
                else:
                    src = w1_deq[idx * P:(idx + 1) * P, :]
            nc.sync.dma_start(out=t[:], in_=src)
            live[("raw", kind, idx)] = t

        def spread_row(row):
            pb = ps_t.tile([P, BANK], F32, tag="tp")
            nc.tensor.matmul(
                pb[:], lhsT=identb[:, row:row + 1].to_broadcast([P, P]), rhs=(vrows1 if row < 2 else vrows2)[:],
                start=True, stop=True,
            )
            dst = bc[:, row * BANK:(row + 1) * BANK]
            if row < 2:
                nc.vector.tensor_copy(
                    out=dst.rearrange("p (u e q) -> p u e q", u=2, e=2),
                    in_=pb[:].rearrange("p (u q e) -> p u e q", u=2, e=2),
                )
            else:
                nc.vector.tensor_copy(out=dst, in_=pb[:])

        def gain_columns():
            g32 = const.tile([P, 256], F32, name="g32")
            nc.vector.tensor_copy(
                out=g32[:].rearrange("p (e q) -> p e q", e=2), in_=grows[:].rearrange("p (q e) -> p e q", e=2)
            )
            pg = ps_t.tile([P, BANK], F32, tag="tp")
            for e in range(2):
                nc.tensor.transpose(pg[:, e * P:(e + 1) * P], g32[:, e * P:(e + 1) * P], ident[:])
            nc.vector.tensor_copy(
                out=gb[:].rearrange("p (w a e) -> p w a e", w=2, e=2),
                in_=pg[:, 0:256].rearrange("p (e r) -> p e r", e=2)[:, :, 0:8].rearrange("p e (w a) -> p w a e", w=2),
            )

        def transpose_words(kind, idx, b):
            if not 0 <= idx < TILES:
                return
            words = live[("raw", kind, idx)][:].bitcast(F32)
            xt = ps_t.tile([P, BANK], F32, tag="tp")
            for s in range(4):
                c0 = (4 * b + s) * P
                nc.tensor.transpose(xt[:, s * P:(s + 1) * P], words[:, c0:c0 + P], ident[:])
            src = xt[:].rearrange("p (g u r) -> p g r u", g=2, u=2)
            if kind in ("W", "w"):
                key = ("grp", kind, idx // 4)
                if key not in live:
                    grouped_w = stagew.tile([P, 4 * D_IN], BF16, tag="grpw", align_bytes=64)
                    live[key] = grouped_w
                dst = live[key][:].bitcast(F32).rearrange("p (g j r u) -> p g j r u", g=4, j=4, u=2)[
                    :, 2 * b:2 * b + 2, idx % 4
                ]
                if b == 1:
                    nc.vector.tensor_copy(out=dst, in_=src)
                else:
                    nc.scalar.copy(out=dst, in_=src)
            else:
                key = ("grp", kind, idx)
                if key not in live:
                    if kind == "a":
                        grouped = stage.tile([P, H], BF16, tag="grpa", align_bytes=64)
                    else:
                        grouped = stage.tile([P, D_IN], BF16, tag="grp", align_bytes=64)
                    live[key] = grouped
                dst = live[key][:].bitcast(F32)[:, b * BANK:(b + 1) * BANK].rearrange(
                    "p (g r u) -> p g r u", g=2, u=2
                )
                nc.scalar.copy(out=dst, in_=src)

        def quantise_weights(kind, n):
            cq, cs = (wq, ws) if kind == "W" else (vq, vs)
            for g in range(PASSES):
                sl = slice(g * H + n * BANK, g * H + (n + 1) * BANK)
                nc.vector.quantize_mx(
                    out=cq[:, sl].bitcast(FP8X4), scales=cs[:, sl],
                    in_=live[("grp", kind, n)][:, g * D_IN:(g + 1) * D_IN],
                )

        def quantise_rows(kind, idx):
            if not 0 <= idx < TILES:
                return
            words = Z_WORDS if kind == "z" else HALF_WORDS
            cq, cs = (zq, zs) if kind == "z" else (aq, ascl)
            sl = slice(idx * words, (idx + 1) * words)
            nc.vector.quantize_mx(out=cq[:, sl].bitcast(FP8X4), scales=cs[:, sl], in_=live[("grp", kind, idx)][:])

        def mx_passes(stg, i, n, first, end):
            if not 0 <= i < TILES:
                return
            if first == 0:
                acc = ps_a.tile([P, BANK], F32, tag="acc")
                live[("acc", stg, i, n)] = acc
            acc = live[("acc", stg, i, n)]
            for g in range(first, end):
                if stg == 1:
                    c0 = i * Z_WORDS + g * P
                    lq, ls, rq, rs = zq, zs, wq, ws
                else:
                    c0 = i * HALF_WORDS + (g % 2) * P
                    lq, ls = (pq, pscl) if g < 2 else (aq, ascl)
                    rq, rs = vq, vs
                sl = slice(c0, c0 + P)
                sr = slice(g * H + n * BANK, g * H + (n + 1) * BANK)
                nc.tensor.matmul_mx(
                    out=acc[:], lhsT=lq[:, sl].bitcast(FP8X4), lhsT_scale=ls[:, sl],
                    rhs=rq[:, sr].bitcast(FP8X4), rhs_scale=rs[:, sr], start=(g == 0), stop=(g == PASSES - 1),
                )
            if end < PASSES:
                return
            if n == 0:
                if stg == 1:
                    y = rows1.tile([P, H], F32, tag="y1")
                else:
                    y = rows2.tile([P, H], F32, tag="y2")
                sums = small.tile([P, 2], F32, tag="sums")
                live[("y", stg, i)] = y
                live[("sums", stg, i)] = sums
            off = (stg - 1) * H + n * BANK
            nc.vector.scalar_tensor_tensor(
                out=live[("y", stg, i)][:, n * BANK:(n + 1) * BANK], in0=acc[:], scalar=1.0,
                in1=bc[:, off:off + BANK], op0=ALU.mult, op1=ALU.add, accum_out=live[("sums", stg, i)][:, n:n + 1],
            )

        def stats(stg, i):
            if not 0 <= i < TILES:
                return
            junk2 = small.tile([P, 2], F32, tag="junk2")
            nmean = small.tile([P, 1], F32, tag="nmean")
            nc.scalar.activation(
                out=junk2[:], in_=live[("sums", stg, i)][:], func=ACT.Identity, scale=-1.0 / H, accum_out=nmean[:]
            )
            junk = junkp.tile([P, H], BF16, tag="junk")
            ssq = small.tile([P, 1], F32, tag="ssq")
            nc.scalar.activation(
                out=junk[:], in_=live[("y", stg, i)][:], func=ACT.Square, bias=nmean[:], scale=1.0, accum_out=ssq[:]
            )
            veps = small.tile([P, 1], F32, tag="veps")
            nc.scalar.activation(out=veps[:], in_=ssq[:], func=ACT.Identity, scale=1.0 / H, bias=eps[:])
            live[("nmean", stg, i)] = nmean
            live[("veps", stg, i)] = veps

        def rstd_of(stg, i):
            if not 0 <= i < TILES:
                return
            rstd = small.tile([P, 1], F32, tag="rstd")
            nc.gpsimd.tensor_tensor(out=rstd[:], in0=live[("veps", stg, i)][:], in1=mhalf[:], op=ALU.pow)
            live[("rstd", stg, i)] = rstd
            if stg == 1:
                y = live[("y", 1, i)]
                nc.gpsimd.tensor_scalar(
                    out=y[:], in0=y[:], scalar1=live[("nmean", 1, i)][:], scalar2=rstd[:], op0=ALU.add, op1=ALU.mult
                )

        def transpose_rows(i, g):
            if not 0 <= i < TILES:
                return
            tp = ps_t.tile([P, BANK], F32, tag="tp")
            for v in range(4):
                blk = 4 * g + v
                nc.tensor.transpose(tp[:, v * P:(v + 1) * P], live[("y", 1, i)][:, blk * P:(blk + 1) * P], ident[:])
            if g == 0:
                planar = plan.tile([P, H], BF16, tag="planar")
                live[("planar", i)] = planar
            for v in range(4):
                blk = 4 * g + v
                nc.scalar.activation(
                    out=live[("planar", i)][:, blk * P:(blk + 1) * P], in_=tp[:, v * P:(v + 1) * P],
                    func=ACT.Identity, scale=gb[:, blk:blk + 1], bias=gb[:, 8 + blk:9 + blk],
                )

        def regroup(i):
            if not 0 <= i < TILES:
                return
            gp = plan.tile([P, H], BF16, tag="gp", align_bytes=64)
            nc.vector.tensor_copy(
                out=gp[:].rearrange("p (g c t) -> p g c t", g=2, t=4),
                in_=live[("planar", i)][:].rearrange("p (g t c) -> p g c t", g=2, t=4),
            )
            sl = slice(i * HALF_WORDS, (i + 1) * HALF_WORDS)
            nc.vector.quantize_mx(out=pq[:, sl].bitcast(FP8X4), scales=pscl[:, sl], in_=gp[:])

        def gain(i):
            if not 0 <= i < TILES:
                return
            t2 = rows3.tile([P, H], F32, tag="t2")
            nc.vector.scalar_tensor_tensor(
                out=t2[:], in0=live[("y", 2, i)][:], scalar=live[("nmean", 2, i)][:], in1=bc[:, 2 * H:3 * H],
                op0=ALU.add, op1=ALU.mult,
            )
            live[("t2", i)] = t2

        def shift(i):
            if not 0 <= i < TILES:
                return
            t2 = live[("t2", i)]
            nc.vector.scalar_tensor_tensor(
                out=t2[:], in0=t2[:], scalar=live[("rstd", 2, i)][:], in1=bc[:, 3 * H:4 * H], op0=ALU.mult, op1=ALU.add
            )

        def gelu_store(i):
            if not 0 <= i < TILES:
                return
            t2 = live[("t2", i)]
            nc.scalar.activation(out=t2[:], in_=t2[:], func=ACT.Gelu)
            nc.sync.dma_start(out=out[i * P:(i + 1) * P, :], in_=t2[:])

        for j in range(TILES):
            load("W", j)
        for r in range(-AHEAD_Z, TILES - AHEAD_A):
            if r + AHEAD_Z < TILES:
                load("z", r + AHEAD_Z)
            if r + AHEAD_A >= 0:
                load("a", r + AHEAD_A)
            for j in (2 * (r + AHEAD_Z), 2 * (r + AHEAD_Z) + 1):
                if j < TILES:
                    load("w", j)

        for j in range(TILES):
            transpose_words("W", j, 0)
            transpose_words("W", j, 1)
            if j == 1:
                spread_row(0)
                spread_row(1)
                gain_columns()
            if j >= 2:
                spread_row(j)
            if j == 4:
                quantise_weights("W", 0)

        for r in range(-AHEAD_Z, TILES + DRAIN_ROUNDS):
            w_first = 2 * (r + AHEAD_Z)
            m = r + AHEAD_M1
            mx_passes(2, r, 0, 0, PASSES)
            regroup(r + 1)
            transpose_words("z", r + AHEAD_Z, 0)
            rstd_of(2, r - 1)
            transpose_words("z", r + AHEAD_Z, 1)
            if w_first == 0:
                quantise_weights("W", 1)
            elif w_first in (4, 8):
                quantise_weights("w", w_first // 4 - 1)
            mx_passes(2, r, 1, 0, PASSES)
            stats(1, m - 1)
            rstd_of(1, m - 1)
            gelu_store(r - 2)
            mx_passes(1, m, 0, 0, 1)
            transpose_words("a", r + AHEAD_A, 0)
            mx_passes(1, m, 0, 1, 2)
            transpose_words("w", w_first, 0)
            mx_passes(1, m, 0, 2, 3)
            transpose_words("w", w_first, 1)
            mx_passes(1, m, 0, 3, PASSES)
            transpose_rows(r + AHEAD_ROWS, 0)
            quantise_rows("z", r + AHEAD_Z)
            stats(2, r)
            mx_passes(1, m, 1, 0, 1)
            transpose_words("w", w_first + 1, 0)
            mx_passes(1, m, 1, 1, 2)
            transpose_words("w", w_first + 1, 1)
            mx_passes(1, m, 1, 2, PASSES)
            quantise_rows("a", r + AHEAD_A)
            shift(r - 1)
            gain(r)
            transpose_rows(r + AHEAD_ROWS, 1)
